import numpy as np
import ml_dtypes


def mxq(x, axis, fmt="e4m3"):
    dtype, down = {"e4m3": (ml_dtypes.float8_e4m3fn, 7), "e5m2": (ml_dtypes.float8_e5m2, 14)}[fmt]
    v = np.moveaxis(np.asarray(x, np.float32).astype(ml_dtypes.bfloat16).astype(np.float64), axis, -1)
    blocks = v.reshape(v.shape[:-1] + (-1, 32))
    amax = np.abs(blocks).max(-1, keepdims=True)
    byte = np.maximum(np.where(amax > 0, np.frexp(amax)[1] - 1 + 127, 0) - down, 1)
    scale = np.exp2(byte - 127.0)
    codes = (blocks / scale).astype(np.float32).astype(dtype).astype(np.float64)
    return np.moveaxis((codes * scale).reshape(v.shape), -1, axis)


WIDE = False


def mx_kscale(k):
    if not WIDE:
        return np.ones(k)
    levels = np.array([10, -10, 5, -5, 0])
    a = np.random.permutation(np.resize(levels, k // 512 * 4)).reshape(k // 512, 4)
    idx = np.arange(k)
    return np.exp2(a[idx // 512, idx % 128 // 32])


BF16 = ml_dtypes.bfloat16


def bf(x):
    return np.asarray(x, np.float32).astype(BF16)


def f64(x):
    return np.asarray(x).astype(np.float64)


E2M1 = np.array([0.0, 0.5, 1.0, 1.5, 2.0, 3.0, 4.0, 6.0, -0.0, -0.5, -1.0, -1.5, -2.0, -3.0, -4.0, -6.0])


def pack_weight(w, fmt):
    k, n = w.shape
    w = f64(bf(w)).reshape(k // 32, 32, n)
    amax = np.abs(w).max(1)
    if fmt == "e4m3":
        byte = np.frexp(amax)[1] - 1 + 127 - 7
    else:
        mant, ex = np.frexp(amax / 6.0)
        byte = np.where(mant > 0.5, ex, ex - 1) + 127
    byte = np.clip(np.where(amax > 0, byte, 1), 1, 254)
    scaled = (w * np.exp2(127.0 - byte)[:, None, :]).reshape(k, n).astype(np.float32)
    by_word = np.ascontiguousarray(scaled.reshape(k // 512, 128, 4, n).transpose(0, 1, 3, 2))
    if fmt == "e4m3":
        words = by_word.astype(ml_dtypes.float8_e4m3fn).view(np.uint8)
    else:
        c = by_word.astype(ml_dtypes.float4_e2m1fn).view(np.uint8) & 0xF
        words = c[..., 0::2] | (c[..., 1::2] << 4)
    return np.ascontiguousarray(words), np.ascontiguousarray(byte.astype(np.uint8).reshape(k // 512, 16, n))


def unpack_weight(words, scales, fmt):
    g, p, n, _ = words.shape
    if fmt == "e4m3":
        vals = np.ascontiguousarray(words).view(ml_dtypes.float8_e4m3fn).astype(np.float64)
    else:
        nib = np.empty((g, p, n, 4), np.uint8)
        nib[..., 0::2] = words & 0xF
        nib[..., 1::2] = words >> 4
        vals = E2M1[nib]
    vals = vals * np.repeat(np.exp2(scales.astype(np.float64) - 127.0), 8, axis=1)[..., None]
    return vals.transpose(0, 1, 3, 2).reshape(g * 512, n)


B, T, I, H = 128, 8, 1024, 1024
FMT = "e4m3"


def sigmoid(v):
    return 1.0 / (1.0 + np.exp(-v))


def setup_inputs():
    s = mx_kscale(I)
    d = {"inputs": bf(np.random.standard_normal((B, T, I)) * s),
         "h0": bf(np.random.standard_normal((1, B, H))),
         "c0": bf(np.random.standard_normal((1, B, H)))}
    for ni, nh in (("ii", "hi"), ("if_", "hf"), ("io", "ho"), ("ig", "hg")):
        w = np.random.standard_normal((H, I)) / np.sqrt(I) / s[None, :]
        words, scales = pack_weight(np.ascontiguousarray(w.T), FMT)
        d["w_" + ni + "_words"] = words
        d["w_" + ni + "_scales"] = scales
        d["b_" + ni] = bf(np.random.standard_normal((H, 1)) * 0.3)
        d["w_" + nh] = bf(np.random.standard_normal((H, H)) * 0.7 / np.sqrt(H))
        d["b_" + nh] = bf(np.random.standard_normal((H, 1)) * 0.3)
    return d


def reference(inputs, h0, c0, w_ii_words, w_ii_scales, b_ii, w_hi, b_hi, w_if__words, w_if__scales, b_if_, w_hf, b_hf, w_io_words, w_io_scales, b_io, w_ho, b_ho, w_ig_words, w_ig_scales, b_ig, w_hg, b_hg):
    xq = mxq(f64(inputs), 2, "e4m3")
    h0s = f64(h0)[0]
    c0s = f64(c0)[0]
    zi = (xq @ unpack_weight(w_ii_words, w_ii_scales, FMT)) + (h0s @ f64(w_hi).T)[:, None, :] + f64(b_ii)[:, 0] + f64(b_hi)[:, 0]
    zf = (xq @ unpack_weight(w_if__words, w_if__scales, FMT)) + (h0s @ f64(w_hf).T)[:, None, :] + f64(b_if_)[:, 0] + f64(b_hf)[:, 0]
    zg = (xq @ unpack_weight(w_ig_words, w_ig_scales, FMT)) + (h0s @ f64(w_hg).T)[:, None, :] + f64(b_ig)[:, 0] + f64(b_hg)[:, 0]
    zo = (xq @ unpack_weight(w_io_words, w_io_scales, FMT)) + (h0s @ f64(w_ho).T)[:, None, :] + f64(b_io)[:, 0] + f64(b_ho)[:, 0]
    i = sigmoid(zi)
    f = sigmoid(zf)
    g = np.tanh(zg)
    o = sigmoid(zo)
    c_next = f * c0s[:, None, :] + i * g
    h_next = o * np.tanh(c_next)
    hidden_seq = np.transpose(h_next, (1, 0, 2))
    h_last = hidden_seq[-1][None]
    c_last = c_next[:, -1][None]
    return hidden_seq, h_last, c_last

@@ -1,0 +1,298 @@
+from contextlib import ExitStack
+
+import concourse.mybir as mybir
+from concourse.masks import make_identity
+
+F32 = mybir.dt.float32
+BF16 = mybir.dt.bfloat16
+I32 = mybir.dt.int32
+U32 = mybir.dt.uint32
+U8 = mybir.dt.uint8
+FP8X4 = mybir.dt.float8_e4m3fn_x4
+ACT = mybir.ActivationFunctionType
+ALU = mybir.AluOpType
+
+P = 128
+STEPS = 8
+FEATURES = 1024
+HIDDEN = 1024
+GATES = 4
+HALVES = 2
+K_PASS = 4 * P
+PASSES = FEATURES // K_PASS
+CHUNK = 256
+CHUNKS = HIDDEN // CHUNK
+ROW_TILES = CHUNK // P
+BANK = 512
+WORD_TILES = HIDDEN // 2 // P
+K_SLICES = HIDDEN // P
+DUO = 2
+DUOS = STEPS // DUO
+
+FLOPS = 2 * P * STEPS * FEATURES * GATES * HIDDEN + 2 * P * HIDDEN * GATES * HIDDEN
+
+
+def tile_naivelstm_pa_kernel(
+    tc,
+    inputs, h0, c0,
+    w_ii_words, w_ii_scales, b_ii, w_hi, b_hi,
+    w_if__words, w_if__scales, b_if_, w_hf, b_hf,
+    w_io_words, w_io_scales, b_io, w_ho, b_ho,
+    w_ig_words, w_ig_scales, b_ig, w_hg, b_hg,
+    out_0, out_1, out_2,
+):
+    nc = tc.nc
+    words_in = [w_ii_words, w_if__words, w_io_words, w_ig_words]
+    scales_in = [w_ii_scales, w_if__scales, w_io_scales, w_ig_scales]
+    hidden_in = [w_hi, w_hf, w_ho, w_hg]
+    bias_in = [(b_ii, b_hi), (b_if_, b_hf), (b_io, b_ho), (b_ig, b_hg)]
+
+    with ExitStack() as ctx:
+        keep = ctx.enter_context(tc.tile_pool(name="keep", bufs=1))
+        rows_pool = ctx.enter_context(tc.tile_pool(name="rows", bufs=3 * GATES))
+        turned_pool = ctx.enter_context(tc.tile_pool(name="turned", bufs=6))
+        stage = ctx.enter_context(tc.tile_pool(name="stage", bufs=3))
+        gates_pool = ctx.enter_context(tc.tile_pool(name="gates", bufs=5))
+        banks = ctx.enter_context(tc.psum_pool(name="banks", bufs=6))
+        hidden_banks = ctx.enter_context(tc.psum_pool(name="hidden_banks", bufs=1))
+
+        ident = keep.tile([P, P], F32, name="ident")
+        make_identity(nc, ident[:])
+        ones = keep.tile([P, P], BF16, name="ones")
+        nc.vector.memset(ones[:], 1.0)
+        bias_rows = keep.tile([P, GATES, HIDDEN], BF16, name="bias_rows")
+        nc.vector.memset(bias_rows[:].rearrange("p q n -> p (q n)").bitcast(I32), 0)
+        planes = keep.tile([P, GATES, PASSES, HIDDEN], U8, name="planes", align_bytes=64)
+        nc.vector.memset(planes[:].rearrange("p q g n -> p (q g n)").bitcast(I32), 0)
+
+        for q in range(GATES):
+            for r in range(2):
+                nc.gpsimd.dma_start(out=bias_rows[r : r + 1, q, :], in_=bias_in[q][r].rearrange("n o -> o n"))
+
+        h0_sb = keep.tile([P, HIDDEN], BF16, name="h0_sb")
+        nc.sync.dma_start(out=h0_sb[:], in_=h0[0])
+
+        hidden_rows = {}
+
+        def load_hidden_rows(c):
+            for q in range(GATES):
+                rows = rows_pool.tile([P, ROW_TILES, HIDDEN], BF16, name="rows", tag="rows")
+                nc.sync.dma_start(
+                    out=rows[:],
+                    in_=hidden_in[q][c * CHUNK : (c + 1) * CHUNK, :].rearrange("(a p) k -> p a k", p=P),
+                )
+                hidden_rows[(c, q)] = rows
+
+        w_codes = {}
+
+        def load_codes(c):
+            for q in range(GATES):
+                codes = keep.tile([P, PASSES, CHUNK], U32, name="w_codes_%d_%d" % (c, q), align_bytes=64)
+                packed = words_in[q].rearrange("g p n t -> p g (n t)")
+                nc.sync.dma_start(
+                    out=codes[:].bitcast(I32),
+                    in_=packed[:, :, 4 * c * CHUNK : 4 * (c + 1) * CHUNK].bitcast(I32),
+                )
+                w_codes[(c, q)] = codes
+
+        x_duos = {}
+
+        def load_inputs(d):
+            x_duos[d] = keep.tile([P, DUO, FEATURES], BF16, name="x_duo_%d" % d)
+            nc.sync.dma_start(out=x_duos[d][:], in_=inputs[:, DUO * d : DUO * (d + 1), :])
+
+        load_hidden_rows(0)
+        load_inputs(0)
+        for q in range(GATES):
+            for quad in range(4):
+                nc.sync.dma_start(
+                    out=planes[32 * quad : 32 * quad + 4, q, :, :].bitcast(I32),
+                    in_=scales_in[q][:, 4 * quad : 4 * quad + 4, :].rearrange("g r n -> r g n").bitcast(I32),
+                )
+        load_codes(0)
+        c0_bf = keep.tile([P, HIDDEN], BF16, name="c0_bf")
+        nc.sync.dma_start(out=c0_bf[:], in_=c0[0])
+        load_inputs(1)
+        load_hidden_rows(1)
+        load_inputs(2)
+        load_inputs(3)
+        load_codes(1)
+        for c in range(2, CHUNKS):
+            load_hidden_rows(c)
+            load_codes(c)
+
+        def turn_h0():
+            bank = banks.tile([P, BANK], F32, name="h0_bank", tag="bank")
+            for w in range(WORD_TILES):
+                nc.tensor.transpose(bank[:, w * P : (w + 1) * P], h0_sb[:].bitcast(F32)[:, w * P : (w + 1) * P], ident[:])
+            h0_t = keep.tile([P, WORD_TILES * P], F32, name="h0_t")
+            nc.vector.tensor_copy(out=h0_t[:], in_=bank[:])
+            return h0_t
+
+        turned = {}
+
+        def turn_hidden_rows(c, w, half):
+            bank = banks.tile([P, BANK], F32, name="rows_bank", tag="bank")
+            for s in range(2):
+                for a in range(ROW_TILES):
+                    col = (s * ROW_TILES + a) * P
+                    rows = hidden_rows[(c, 2 * half + s)]
+                    nc.tensor.transpose(
+                        bank[:, col : col + P], rows[:, a, :].bitcast(F32)[:, w * P : (w + 1) * P], ident[:]
+                    )
+            if half == 0:
+                turned[(c, w)] = turned_pool.tile([P, GATES * CHUNK], F32, name="turned", tag="turned")
+            nc.scalar.copy(out=turned[(c, w)][:, half * BANK : (half + 1) * BANK], in_=bank[:])
+
+        hidden_sum = {}
+
+        def close_hidden_sum(c, half):
+            nc.tensor.matmul(
+                out=hidden_sum[(c, half)][:],
+                lhsT=ones[:],
+                rhs=bias_rows[:, 2 * half : 2 * half + 2, c * CHUNK : (c + 1) * CHUNK],
+                start=False,
+                stop=True,
+            )
+
+        def add_hidden_slice(c, k, half):
+            w, e = divmod(k, 2)
+            if k == 0:
+                hidden_sum[(c, half)] = hidden_banks.tile([P, BANK], F32, name="hidden_sum_%d" % half)
+            h0_pairs = h0_t[:].bitcast(BF16).rearrange("p (b e) -> p b e", e=2)
+            w_pairs = turned[(c, w)][:].bitcast(BF16).rearrange("p (n e) -> p n e", e=2)
+            nc.tensor.matmul(
+                out=hidden_sum[(c, half)][:],
+                lhsT=h0_pairs[:, w * P : (w + 1) * P, e],
+                rhs=w_pairs[:, half * BANK : (half + 1) * BANK, e],
+                start=(k == 0),
+                stop=False,
+            )
+
+        def hidden_sum_out(c):
+            hidden_sb = stage.tile([P, GATES * CHUNK], F32, name="hidden_sb")
+            for half in range(HALVES):
+                nc.vector.tensor_copy(out=hidden_sb[:, half * BANK : (half + 1) * BANK], in_=hidden_sum[(c, half)][:])
+            return hidden_sb
+
+        def turn_inputs(t):
+            x_words = x_duos[t // DUO][:, t % DUO, :].bitcast(F32)
+            bank = banks.tile([P, BANK], F32, name="x_bank", tag="bank")
+            for g in range(PASSES):
+                for u in range(2):
+                    col = (2 * g + u) * P
+                    nc.tensor.transpose(
+                        bank[:, col : col + P], x_words[:, 2 * P * g + u : 2 * P * (g + 1) : 2], ident[:]
+                    )
+            grouped = stage.tile([P, FEATURES], BF16, name="grouped", align_bytes=64)
+            nc.vector.tensor_copy(
+                out=grouped[:].bitcast(F32).rearrange("p (g b u) -> p g b u", g=PASSES, u=2),
+                in_=bank[:].rearrange("p (g u b) -> p g b u", g=PASSES, u=2),
+            )
+            return grouped
+
+        x_codes = {}
+        x_scales = {}
+
+        def quantise_inputs(t, grouped):
+            x_codes[t] = keep.tile([P, PASSES * P], U32, name="x_codes_%d" % t, align_bytes=64)
+            x_scales[t] = keep.tile([P, PASSES * P], U8, name="x_scales_%d" % t, align_bytes=64)
+            nc.vector.quantize_mx(out=x_codes[t][:].bitcast(FP8X4), scales=x_scales[t][:], in_=grouped[:])
+
+        def prepare_inputs(d):
+            grouped = [turn_inputs(t) for t in range(DUO * d, DUO * (d + 1))]
+            for i in range(DUO):
+                quantise_inputs(DUO * d + i, grouped[i])
+
+        def gate_sums(c, t, hidden_sb, z_sb):
+            for half in range(HALVES):
+                bank = banks.tile([P, BANK], F32, name="z_bank", tag="bank")
+                for s in range(2):
+                    q = 2 * half + s
+                    for g in range(PASSES):
+                        nc.tensor.matmul_mx(
+                            out=bank[:, s * CHUNK : (s + 1) * CHUNK],
+                            lhsT=x_codes[t][:, g * P : (g + 1) * P].bitcast(FP8X4),
+                            lhsT_scale=x_scales[t][:, g * P : (g + 1) * P],
+                            rhs=w_codes[(c, q)][:, g, :].bitcast(FP8X4),
+                            rhs_scale=planes[:, q, g, c * CHUNK : (c + 1) * CHUNK],
+                            start=(g == 0),
+                            stop=(g == PASSES - 1),
+                        )
+                nc.vector.tensor_tensor(
+                    out=z_sb[:, t % DUO, half * BANK : (half + 1) * BANK],
+                    in0=bank[:],
+                    in1=hidden_sb[:, half * BANK : (half + 1) * BANK],
+                    op=ALU.add,
+                )
+
+        def gate(z_sb, q):
+            return z_sb[:, :, q * CHUNK : (q + 1) * CHUNK]
+
+        def activate(z_sb):
+            nc.scalar.activation(out=z_sb[:, :, 0 : 3 * CHUNK], in_=z_sb[:, :, 0 : 3 * CHUNK], func=ACT.Sigmoid)
+            nc.scalar.activation(out=gate(z_sb, 3), in_=gate(z_sb, 3), func=ACT.Tanh)
+
+        def cell_state(c, z_sb):
+            c0_chunk = c0_sb[:, c * CHUNK : (c + 1) * CHUNK].unsqueeze(1).to_broadcast([P, DUO, CHUNK])
+            nc.gpsimd.tensor_tensor(out=gate(z_sb, 1), in0=gate(z_sb, 1), in1=c0_chunk, op=ALU.mult)
+            nc.gpsimd.tensor_tensor(out=gate(z_sb, 0), in0=gate(z_sb, 0), in1=gate(z_sb, 3), op=ALU.mult)
+            cell = stage.tile([P, DUO, CHUNK], F32, name="cell")
+            nc.gpsimd.tensor_tensor(out=cell[:], in0=gate(z_sb, 1), in1=gate(z_sb, 0), op=ALU.add)
+            return cell
+
+        def cell_tanh(z_sb, cell):
+            nc.scalar.activation(out=gate(z_sb, 3), in_=cell[:], func=ACT.Tanh)
+
+        def hidden_state(c, d, z_sb, cell):
+            cols = slice(c * CHUNK, (c + 1) * CHUNK)
+            h_sb = stage.tile([P, DUO, CHUNK], F32, name="h_sb")
+            nc.vector.tensor_tensor(out=h_sb[:], in0=gate(z_sb, 2), in1=gate(z_sb, 3), op=ALU.mult)
+            nc.sync.dma_start(out=out_0[DUO * d : DUO * (d + 1), :, cols].rearrange("t b n -> b t n"), in_=h_sb[:])
+            if d == DUOS - 1:
+                nc.sync.dma_start(out=out_1[0, :, cols], in_=h_sb[:, DUO - 1, :])
+                nc.sync.dma_start(out=out_2[0, :, cols], in_=cell[:, DUO - 1, :])
+
+        h0_t = turn_h0()
+        for half in range(HALVES):
+            for w in range(WORD_TILES):
+                turn_hidden_rows(0, w, half)
+        for half in range(HALVES):
+            for k in range(K_SLICES):
+                add_hidden_slice(0, k, half)
+            close_hidden_sum(0, half)
+        prepare_inputs(0)
+        c0_sb = keep.tile([P, HIDDEN], F32, name="c0_sb")
+        nc.vector.tensor_copy(out=c0_sb[:], in_=c0_bf[:])
+        for half in range(HALVES):
+            turn_hidden_rows(1, 0, half)
+
+        rounds = CHUNKS * DUOS
+        z_of = {}
+        cell_of = {}
+        hidden_sb = None
+        for j in range(rounds + 2):
+            if j < rounds:
+                c, d = divmod(j, DUOS)
+                if d == 0:
+                    hidden_sb = hidden_sum_out(c)
+                z_of[j] = gates_pool.tile([P, DUO, GATES * CHUNK], F32, name="z_sb", tag="z_sb")
+                for t in range(DUO * d, DUO * (d + 1)):
+                    gate_sums(c, t, hidden_sb, z_of[j])
+                    if c + 1 < CHUNKS:
+                        for half in range(HALVES):
+                            add_hidden_slice(c + 1, t, half)
+                            if t == STEPS - 1:
+                                close_hidden_sum(c + 1, half)
+                if c == 0 and d + 1 < DUOS:
+                    prepare_inputs(d + 1)
+                next_tile = WORD_TILES * (c + 1) + d + 1
+                if next_tile < WORD_TILES * CHUNKS:
+                    for half in range(HALVES):
+                        turn_hidden_rows(next_tile // WORD_TILES, next_tile % WORD_TILES, half)
+                activate(z_of[j])
+                cell_of[j] = cell_state(c, z_of[j])
+            if 1 <= j <= rounds:
+                cell_tanh(z_of[j - 1], cell_of[j - 1])
+            if j >= 2:
+                hidden_state((j - 2) // DUOS, (j - 2) % DUOS, z_of[j - 2], cell_of[j - 2])

@@ -55,6 +55,7 @@ def tile_naivelstm_pa_kernel(
         gates_pool = ctx.enter_context(tc.tile_pool(name="gates", bufs=5))
         banks = ctx.enter_context(tc.psum_pool(name="banks", bufs=6))
         hidden_banks = ctx.enter_context(tc.psum_pool(name="hidden_banks", bufs=1))
+        ctx.enter_context(tc.manual_schedule())
 
         ident = keep.tile([P, P], F32, name="ident")
         make_identity(nc, ident[:])
@@ -103,6 +104,7 @@ def tile_naivelstm_pa_kernel(
 
         load_hidden_rows(0)
         load_inputs(0)
+        load_hidden_rows(1)
         for q in range(GATES):
             for quad in range(4):
                 nc.sync.dma_start(
@@ -110,10 +112,9 @@ def tile_naivelstm_pa_kernel(
                     in_=scales_in[q][:, 4 * quad : 4 * quad + 4, :].rearrange("g r n -> r g n").bitcast(I32),
                 )
         load_codes(0)
-        c0_bf = keep.tile([P, HIDDEN], BF16, name="c0_bf")
-        nc.sync.dma_start(out=c0_bf[:], in_=c0[0])
+        c0_sb = keep.tile([P, HIDDEN], BF16, name="c0_sb")
+        nc.sync.dma_start(out=c0_sb[:], in_=c0[0])
         load_inputs(1)
-        load_hidden_rows(1)
         load_inputs(2)
         load_inputs(3)
         load_codes(1)
@@ -262,8 +263,6 @@ def tile_naivelstm_pa_kernel(
                 add_hidden_slice(0, k, half)
             close_hidden_sum(0, half)
         prepare_inputs(0)
-        c0_sb = keep.tile([P, HIDDEN], F32, name="c0_sb")
-        nc.vector.tensor_copy(out=c0_sb[:], in_=c0_bf[:])
         for half in range(HALVES):
             turn_hidden_rows(1, 0, half)
 
@@ -272,8 +271,20 @@ def tile_naivelstm_pa_kernel(
         cell_of = {}
         hidden_sb = None
         for j in range(rounds + 2):
+            c, d = divmod(j, DUOS)
+            if 1 <= j <= rounds:
+                activate(z_of[j - 1])
+                cell_of[j - 1] = cell_state((j - 1) // DUOS, z_of[j - 1])
             if j < rounds:
-                c, d = divmod(j, DUOS)
+                next_tile = j + WORD_TILES + 1
+                if next_tile < WORD_TILES * CHUNKS:
+                    for half in range(HALVES):
+                        turn_hidden_rows(next_tile // WORD_TILES, next_tile % WORD_TILES, half)
+                if c == 0 and d + 1 < DUOS:
+                    prepare_inputs(d + 1)
+            if j >= 2:
+                cell_tanh(z_of[j - 2], cell_of[j - 2])
+            if j < rounds:
                 if d == 0:
                     hidden_sb = hidden_sum_out(c)
                 z_of[j] = gates_pool.tile([P, DUO, GATES * CHUNK], F32, name="z_sb", tag="z_sb")
@@ -284,15 +295,5 @@ def tile_naivelstm_pa_kernel(
                             add_hidden_slice(c + 1, t, half)
                             if t == STEPS - 1:
                                 close_hidden_sum(c + 1, half)
-                if c == 0 and d + 1 < DUOS:
-                    prepare_inputs(d + 1)
-                next_tile = WORD_TILES * (c + 1) + d + 1
-                if next_tile < WORD_TILES * CHUNKS:
-                    for half in range(HALVES):
-                        turn_hidden_rows(next_tile // WORD_TILES, next_tile % WORD_TILES, half)
-                activate(z_of[j])
-                cell_of[j] = cell_state(c, z_of[j])
-            if 1 <= j <= rounds:
-                cell_tanh(z_of[j - 1], cell_of[j - 1])
             if j >= 2:
                 hidden_state((j - 2) // DUOS, (j - 2) % DUOS, z_of[j - 2], cell_of[j - 2])

@@ -61,14 +61,17 @@ def tile_naivelstm_pa_kernel(
         make_identity(nc, ident[:])
         ones = keep.tile([P, P], BF16, name="ones")
         nc.vector.memset(ones[:], 1.0)
-        bias_rows = keep.tile([P, GATES, HIDDEN], BF16, name="bias_rows")
-        nc.vector.memset(bias_rows[:].rearrange("p q n -> p (q n)").bitcast(I32), 0)
         planes = keep.tile([P, GATES, PASSES, HIDDEN], U8, name="planes", align_bytes=64)
         nc.vector.memset(planes[:].rearrange("p q g n -> p (q g n)").bitcast(I32), 0)
+        bias_rows = keep.tile([P, GATES, HIDDEN], BF16, name="bias_rows")
+        nc.vector.memset(bias_rows[:].rearrange("p q n -> p (q n)").bitcast(I32), 0)
 
         for q in range(GATES):
-            for r in range(2):
-                nc.gpsimd.dma_start(out=bias_rows[r : r + 1, q, :], in_=bias_in[q][r].rearrange("n o -> o n"))
+            for quad in range(4):
+                nc.gpsimd.dma_start(
+                    out=planes[32 * quad : 32 * quad + 4, q, :, :].bitcast(F32),
+                    in_=scales_in[q][:, 4 * quad : 4 * quad + 4, :].rearrange("g r n -> r g n").bitcast(F32),
+                )
 
         h0_sb = keep.tile([P, HIDDEN], BF16, name="h0_sb")
         nc.sync.dma_start(out=h0_sb[:], in_=h0[0])
@@ -103,14 +106,11 @@ def tile_naivelstm_pa_kernel(
             nc.sync.dma_start(out=x_duos[d][:], in_=inputs[:, DUO * d : DUO * (d + 1), :])
 
         load_hidden_rows(0)
+        for q in range(GATES):
+            for r in range(2):
+                nc.scalar.dma_start(out=bias_rows[r : r + 1, q, :], in_=bias_in[q][r].rearrange("n o -> o n"))
         load_inputs(0)
         load_hidden_rows(1)
-        for q in range(GATES):
-            for quad in range(4):
-                nc.sync.dma_start(
-                    out=planes[32 * quad : 32 * quad + 4, q, :, :].bitcast(I32),
-                    in_=scales_in[q][:, 4 * quad : 4 * quad + 4, :].rearrange("g r n -> r g n").bitcast(I32),
-                )
         load_codes(0)
         c0_sb = keep.tile([P, HIDDEN], BF16, name="c0_sb")
         nc.sync.dma_start(out=c0_sb[:], in_=c0[0])
@@ -186,7 +186,7 @@ def tile_naivelstm_pa_kernel(
                         bank[:, col : col + P], x_words[:, 2 * P * g + u : 2 * P * (g + 1) : 2], ident[:]
                     )
             grouped = stage.tile([P, FEATURES], BF16, name="grouped", align_bytes=64)
-            nc.vector.tensor_copy(
+            nc.scalar.copy(
                 out=grouped[:].bitcast(F32).rearrange("p (g b u) -> p g b u", g=PASSES, u=2),
                 in_=bank[:].rearrange("p (g u b) -> p g b u", g=PASSES, u=2),
             )
@@ -199,11 +199,6 @@ def tile_naivelstm_pa_kernel(
             x_codes[t] = keep.tile([P, PASSES * P], U32, name="x_codes_%d" % t, align_bytes=64)
             x_scales[t] = keep.tile([P, PASSES * P], U8, name="x_scales_%d" % t, align_bytes=64)
             nc.vector.quantize_mx(out=x_codes[t][:].bitcast(FP8X4), scales=x_scales[t][:], in_=grouped[:])
-
-        def prepare_inputs(d):
-            grouped = [turn_inputs(t) for t in range(DUO * d, DUO * (d + 1))]
-            for i in range(DUO):
-                quantise_inputs(DUO * d + i, grouped[i])
 
         def gate_sums(c, t, hidden_sb, z_sb):
             for half in range(HALVES):
@@ -234,12 +229,14 @@ def tile_naivelstm_pa_kernel(
             nc.scalar.activation(out=z_sb[:, :, 0 : 3 * CHUNK], in_=z_sb[:, :, 0 : 3 * CHUNK], func=ACT.Sigmoid)
             nc.scalar.activation(out=gate(z_sb, 3), in_=gate(z_sb, 3), func=ACT.Tanh)
 
-        def cell_state(c, z_sb):
+        def cell_products(c, z_sb):
             c0_chunk = c0_sb[:, c * CHUNK : (c + 1) * CHUNK].unsqueeze(1).to_broadcast([P, DUO, CHUNK])
             nc.gpsimd.tensor_tensor(out=gate(z_sb, 1), in0=gate(z_sb, 1), in1=c0_chunk, op=ALU.mult)
             nc.gpsimd.tensor_tensor(out=gate(z_sb, 0), in0=gate(z_sb, 0), in1=gate(z_sb, 3), op=ALU.mult)
+
+        def cell_state(z_sb):
             cell = stage.tile([P, DUO, CHUNK], F32, name="cell")
-            nc.gpsimd.tensor_tensor(out=cell[:], in0=gate(z_sb, 1), in1=gate(z_sb, 0), op=ALU.add)
+            nc.vector.tensor_tensor(out=cell[:], in0=gate(z_sb, 1), in1=gate(z_sb, 0), op=ALU.add)
             return cell
 
         def cell_tanh(z_sb, cell):
@@ -262,7 +259,11 @@ def tile_naivelstm_pa_kernel(
             for k in range(K_SLICES):
                 add_hidden_slice(0, k, half)
             close_hidden_sum(0, half)
-        prepare_inputs(0)
+        grouped_of = {}
+        for t in range(DUO):
+            grouped_of[t] = turn_inputs(t)
+        for t in range(DUO):
+            quantise_inputs(t, grouped_of[t])
         for half in range(HALVES):
             turn_hidden_rows(1, 0, half)
 
@@ -272,16 +273,15 @@ def tile_naivelstm_pa_kernel(
         hidden_sb = None
         for j in range(rounds + 2):
             c, d = divmod(j, DUOS)
+            more_inputs = j < DUOS - 1
             if 1 <= j <= rounds:
                 activate(z_of[j - 1])
-                cell_of[j - 1] = cell_state((j - 1) // DUOS, z_of[j - 1])
+                cell_products((j - 1) // DUOS, z_of[j - 1])
             if j < rounds:
                 next_tile = j + WORD_TILES + 1
                 if next_tile < WORD_TILES * CHUNKS:
                     for half in range(HALVES):
                         turn_hidden_rows(next_tile // WORD_TILES, next_tile % WORD_TILES, half)
-                if c == 0 and d + 1 < DUOS:
-                    prepare_inputs(d + 1)
             if j >= 2:
                 cell_tanh(z_of[j - 2], cell_of[j - 2])
             if j < rounds:
@@ -295,5 +295,13 @@ def tile_naivelstm_pa_kernel(
                             add_hidden_slice(c + 1, t, half)
                             if t == STEPS - 1:
                                 close_hidden_sum(c + 1, half)
+            if more_inputs:
+                for t in range(DUO * (d + 1), DUO * (d + 2)):
+                    grouped_of[t] = turn_inputs(t)
+            if 1 <= j <= rounds:
+                cell_of[j - 1] = cell_state(z_of[j - 1])
             if j >= 2:
                 hidden_state((j - 2) // DUOS, (j - 2) % DUOS, z_of[j - 2], cell_of[j - 2])
+            if more_inputs:
+                for t in range(DUO * (d + 1), DUO * (d + 2)):
+                    quantise_inputs(t, grouped_of[t])

@@ -49,10 +49,11 @@ def tile_naivelstm_pa_kernel(
 
     with ExitStack() as ctx:
         keep = ctx.enter_context(tc.tile_pool(name="keep", bufs=1))
-        rows_pool = ctx.enter_context(tc.tile_pool(name="rows", bufs=3 * GATES))
+        rows_pool = ctx.enter_context(tc.tile_pool(name="rows", bufs=2 * GATES))
         turned_pool = ctx.enter_context(tc.tile_pool(name="turned", bufs=6))
-        stage = ctx.enter_context(tc.tile_pool(name="stage", bufs=3))
-        gates_pool = ctx.enter_context(tc.tile_pool(name="gates", bufs=5))
+        stage = ctx.enter_context(tc.tile_pool(name="stage", bufs=4))
+        hidden_pool = ctx.enter_context(tc.tile_pool(name="hidden", bufs=2))
+        gates_pool = ctx.enter_context(tc.tile_pool(name="gates", bufs=6))
         banks = ctx.enter_context(tc.psum_pool(name="banks", bufs=6))
         hidden_banks = ctx.enter_context(tc.psum_pool(name="hidden_banks", bufs=1))
         ctx.enter_context(tc.manual_schedule())
@@ -109,14 +110,12 @@ def tile_naivelstm_pa_kernel(
         for q in range(GATES):
             for r in range(2):
                 nc.scalar.dma_start(out=bias_rows[r : r + 1, q, :], in_=bias_in[q][r].rearrange("n o -> o n"))
-        load_inputs(0)
+        for d in range(DUOS):
+            load_inputs(d)
         load_hidden_rows(1)
         load_codes(0)
         c0_sb = keep.tile([P, HIDDEN], BF16, name="c0_sb")
         nc.sync.dma_start(out=c0_sb[:], in_=c0[0])
-        load_inputs(1)
-        load_inputs(2)
-        load_inputs(3)
         load_codes(1)
         for c in range(2, CHUNKS):
             load_hidden_rows(c)
@@ -171,7 +170,7 @@ def tile_naivelstm_pa_kernel(
             )
 
         def hidden_sum_out(c):
-            hidden_sb = stage.tile([P, GATES * CHUNK], F32, name="hidden_sb")
+            hidden_sb = hidden_pool.tile([P, GATES * CHUNK], F32, name="hidden_sb")
             for half in range(HALVES):
                 nc.vector.tensor_copy(out=hidden_sb[:, half * BANK : (half + 1) * BANK], in_=hidden_sum[(c, half)][:])
             return hidden_sb
@@ -225,9 +224,9 @@ def tile_naivelstm_pa_kernel(
         def gate(z_sb, q):
             return z_sb[:, :, q * CHUNK : (q + 1) * CHUNK]
 
-        def activate(z_sb):
-            nc.scalar.activation(out=z_sb[:, :, 0 : 3 * CHUNK], in_=z_sb[:, :, 0 : 3 * CHUNK], func=ACT.Sigmoid)
-            nc.scalar.activation(out=gate(z_sb, 3), in_=gate(z_sb, 3), func=ACT.Tanh)
+        def activate(z_sb, first, last, func):
+            gates = z_sb[:, :, first * CHUNK : (last + 1) * CHUNK]
+            nc.scalar.activation(out=gates, in_=gates, func=func)
 
         def cell_products(c, z_sb):
             c0_chunk = c0_sb[:, c * CHUNK : (c + 1) * CHUNK].unsqueeze(1).to_broadcast([P, DUO, CHUNK])
@@ -259,11 +258,12 @@ def tile_naivelstm_pa_kernel(
             for k in range(K_SLICES):
                 add_hidden_slice(0, k, half)
             close_hidden_sum(0, half)
-        grouped_of = {}
-        for t in range(DUO):
-            grouped_of[t] = turn_inputs(t)
-        for t in range(DUO):
-            quantise_inputs(t, grouped_of[t])
+            steps = range(half * STEPS // HALVES, (half + 1) * STEPS // HALVES)
+            grouped_of = {}
+            for t in steps:
+                grouped_of[t] = turn_inputs(t)
+            for t in steps:
+                quantise_inputs(t, grouped_of[t])
         for half in range(HALVES):
             turn_hidden_rows(1, 0, half)
 
@@ -271,19 +271,19 @@ def tile_naivelstm_pa_kernel(
         z_of = {}
         cell_of = {}
         hidden_sb = None
-        for j in range(rounds + 2):
+        for j in range(rounds + 3):
             c, d = divmod(j, DUOS)
-            more_inputs = j < DUOS - 1
             if 1 <= j <= rounds:
-                activate(z_of[j - 1])
+                activate(z_of[j - 1], 0, 1, ACT.Sigmoid)
+                activate(z_of[j - 1], 3, 3, ACT.Tanh)
                 cell_products((j - 1) // DUOS, z_of[j - 1])
-            if j < rounds:
-                next_tile = j + WORD_TILES + 1
-                if next_tile < WORD_TILES * CHUNKS:
-                    for half in range(HALVES):
-                        turn_hidden_rows(next_tile // WORD_TILES, next_tile % WORD_TILES, half)
-            if j >= 2:
-                cell_tanh(z_of[j - 2], cell_of[j - 2])
+                activate(z_of[j - 1], 2, 2, ACT.Sigmoid)
+            next_tile = j + WORD_TILES + 1
+            if next_tile < WORD_TILES * CHUNKS:
+                for half in range(HALVES):
+                    turn_hidden_rows(next_tile // WORD_TILES, next_tile % WORD_TILES, half)
+            if j >= 3:
+                cell_tanh(z_of[j - 3], cell_of[j - 3])
             if j < rounds:
                 if d == 0:
                     hidden_sb = hidden_sum_out(c)
@@ -295,13 +295,7 @@ def tile_naivelstm_pa_kernel(
                             add_hidden_slice(c + 1, t, half)
                             if t == STEPS - 1:
                                 close_hidden_sum(c + 1, half)
-            if more_inputs:
-                for t in range(DUO * (d + 1), DUO * (d + 2)):
-                    grouped_of[t] = turn_inputs(t)
-            if 1 <= j <= rounds:
-                cell_of[j - 1] = cell_state(z_of[j - 1])
-            if j >= 2:
-                hidden_state((j - 2) // DUOS, (j - 2) % DUOS, z_of[j - 2], cell_of[j - 2])
-            if more_inputs:
-                for t in range(DUO * (d + 1), DUO * (d + 2)):
-                    quantise_inputs(t, grouped_of[t])
+            if 2 <= j <= rounds + 1:
+                cell_of[j - 2] = cell_state(z_of[j - 2])
+            if j >= 3:
+                hidden_state((j - 3) // DUOS, (j - 3) % DUOS, z_of[j - 3], cell_of[j - 3])

@@ -233,22 +233,23 @@ def tile_naivelstm_pa_kernel(
             nc.gpsimd.tensor_tensor(out=gate(z_sb, 1), in0=gate(z_sb, 1), in1=c0_chunk, op=ALU.mult)
             nc.gpsimd.tensor_tensor(out=gate(z_sb, 0), in0=gate(z_sb, 0), in1=gate(z_sb, 3), op=ALU.mult)
 
-        def cell_state(z_sb):
+        def cell_state(c, d, z_sb):
             cell = stage.tile([P, DUO, CHUNK], F32, name="cell")
             nc.vector.tensor_tensor(out=cell[:], in0=gate(z_sb, 1), in1=gate(z_sb, 0), op=ALU.add)
+            if d == DUOS - 1:
+                nc.sync.dma_start(out=out_2[0, :, c * CHUNK : (c + 1) * CHUNK], in_=cell[:, DUO - 1, :])
             return cell
 
         def cell_tanh(z_sb, cell):
             nc.scalar.activation(out=gate(z_sb, 3), in_=cell[:], func=ACT.Tanh)
 
-        def hidden_state(c, d, z_sb, cell):
+        def hidden_state(c, d, z_sb):
             cols = slice(c * CHUNK, (c + 1) * CHUNK)
             h_sb = stage.tile([P, DUO, CHUNK], F32, name="h_sb")
             nc.vector.tensor_tensor(out=h_sb[:], in0=gate(z_sb, 2), in1=gate(z_sb, 3), op=ALU.mult)
             nc.sync.dma_start(out=out_0[DUO * d : DUO * (d + 1), :, cols].rearrange("t b n -> b t n"), in_=h_sb[:])
             if d == DUOS - 1:
                 nc.sync.dma_start(out=out_1[0, :, cols], in_=h_sb[:, DUO - 1, :])
-                nc.sync.dma_start(out=out_2[0, :, cols], in_=cell[:, DUO - 1, :])
 
         h0_t = turn_h0()
         for half in range(HALVES):
@@ -290,12 +291,13 @@ def tile_naivelstm_pa_kernel(
                 z_of[j] = gates_pool.tile([P, DUO, GATES * CHUNK], F32, name="z_sb", tag="z_sb")
                 for t in range(DUO * d, DUO * (d + 1)):
                     gate_sums(c, t, hidden_sb, z_of[j])
-                    if c + 1 < CHUNKS:
-                        for half in range(HALVES):
-                            add_hidden_slice(c + 1, t, half)
-                            if t == STEPS - 1:
-                                close_hidden_sum(c + 1, half)
+                if c + 1 < CHUNKS:
+                    for half in range(HALVES):
+                        for k in range(DUO * d, DUO * (d + 1)):
+                            add_hidden_slice(c + 1, k, half)
+                        if d == DUOS - 1:
+                            close_hidden_sum(c + 1, half)
             if 2 <= j <= rounds + 1:
-                cell_of[j - 2] = cell_state(z_of[j - 2])
+                cell_of[j - 2] = cell_state((j - 2) // DUOS, (j - 2) % DUOS, z_of[j - 2])
             if j >= 3:
-                hidden_state((j - 3) // DUOS, (j - 3) % DUOS, z_of[j - 3], cell_of[j - 3])
+                hidden_state((j - 3) // DUOS, (j - 3) % DUOS, z_of[j - 3])

@@ -131,18 +131,25 @@ def tile_naivelstm_pa_kernel(
 
         turned = {}
 
-        def turn_hidden_rows(c, w, half):
-            bank = banks.tile([P, BANK], F32, name="rows_bank", tag="bank")
-            for s in range(2):
-                for a in range(ROW_TILES):
-                    col = (s * ROW_TILES + a) * P
-                    rows = hidden_rows[(c, 2 * half + s)]
-                    nc.tensor.transpose(
-                        bank[:, col : col + P], rows[:, a, :].bitcast(F32)[:, w * P : (w + 1) * P], ident[:]
-                    )
+        def turn_gate_rows(c, w, q, bank):
+            for a in range(ROW_TILES):
+                col = ((q % 2) * ROW_TILES + a) * P
+                nc.tensor.transpose(
+                    bank[:, col : col + P],
+                    hidden_rows[(c, q)][:, a, :].bitcast(F32)[:, w * P : (w + 1) * P],
+                    ident[:],
+                )
+
+        def turned_out(c, w, half, bank):
             if half == 0:
                 turned[(c, w)] = turned_pool.tile([P, GATES * CHUNK], F32, name="turned", tag="turned")
             nc.scalar.copy(out=turned[(c, w)][:, half * BANK : (half + 1) * BANK], in_=bank[:])
+
+        def turn_hidden_rows(c, w, half):
+            bank = banks.tile([P, BANK], F32, name="rows_bank", tag="bank")
+            for s in range(2):
+                turn_gate_rows(c, w, 2 * half + s, bank)
+            turned_out(c, w, half, bank)
 
         hidden_sum = {}
 
@@ -175,15 +182,13 @@ def tile_naivelstm_pa_kernel(
                 nc.vector.tensor_copy(out=hidden_sb[:, half * BANK : (half + 1) * BANK], in_=hidden_sum[(c, half)][:])
             return hidden_sb
 
-        def turn_inputs(t):
+        def turn_inputs(t, g, bank):
             x_words = x_duos[t // DUO][:, t % DUO, :].bitcast(F32)
-            bank = banks.tile([P, BANK], F32, name="x_bank", tag="bank")
-            for g in range(PASSES):
-                for u in range(2):
-                    col = (2 * g + u) * P
-                    nc.tensor.transpose(
-                        bank[:, col : col + P], x_words[:, 2 * P * g + u : 2 * P * (g + 1) : 2], ident[:]
-                    )
+            for u in range(2):
+                col = (2 * g + u) * P
+                nc.tensor.transpose(bank[:, col : col + P], x_words[:, 2 * P * g + u : 2 * P * (g + 1) : 2], ident[:])
+
+        def group_inputs(bank):
             grouped = stage.tile([P, FEATURES], BF16, name="grouped", align_bytes=64)
             nc.scalar.copy(
                 out=grouped[:].bitcast(F32).rearrange("p (g b u) -> p g b u", g=PASSES, u=2),
@@ -255,16 +260,20 @@ def tile_naivelstm_pa_kernel(
         for half in range(HALVES):
             for w in range(WORD_TILES):
                 turn_hidden_rows(0, w, half)
+        grouped_of = {}
         for half in range(HALVES):
             for k in range(K_SLICES):
                 add_hidden_slice(0, k, half)
+                t, g = divmod(half * K_SLICES + k, PASSES)
+                if g == 0:
+                    x_bank = banks.tile([P, BANK], F32, name="x_bank", tag="bank")
+                turn_inputs(t, g, x_bank)
+                if g == PASSES - 1:
+                    grouped_of[t] = group_inputs(x_bank)
+                    if t > 0:
+                        quantise_inputs(t - 1, grouped_of[t - 1])
             close_hidden_sum(0, half)
-            steps = range(half * STEPS // HALVES, (half + 1) * STEPS // HALVES)
-            grouped_of = {}
-            for t in steps:
-                grouped_of[t] = turn_inputs(t)
-            for t in steps:
-                quantise_inputs(t, grouped_of[t])
+        quantise_inputs(STEPS - 1, grouped_of[STEPS - 1])
         for half in range(HALVES):
             turn_hidden_rows(1, 0, half)
 
@@ -279,10 +288,6 @@ def tile_naivelstm_pa_kernel(
                 activate(z_of[j - 1], 3, 3, ACT.Tanh)
                 cell_products((j - 1) // DUOS, z_of[j - 1])
                 activate(z_of[j - 1], 2, 2, ACT.Sigmoid)
-            next_tile = j + WORD_TILES + 1
-            if next_tile < WORD_TILES * CHUNKS:
-                for half in range(HALVES):
-                    turn_hidden_rows(next_tile // WORD_TILES, next_tile % WORD_TILES, half)
             if j >= 3:
                 cell_tanh(z_of[j - 3], cell_of[j - 3])
             if j < rounds:
@@ -292,9 +297,16 @@ def tile_naivelstm_pa_kernel(
                 for t in range(DUO * d, DUO * (d + 1)):
                     gate_sums(c, t, hidden_sb, z_of[j])
                 if c + 1 < CHUNKS:
+                    next_c, next_w = divmod(j + WORD_TILES + 1, WORD_TILES)
                     for half in range(HALVES):
-                        for k in range(DUO * d, DUO * (d + 1)):
-                            add_hidden_slice(c + 1, k, half)
+                        if next_c < CHUNKS:
+                            rows_bank = banks.tile([P, BANK], F32, name="rows_bank", tag="bank")
+                        for s in range(2):
+                            add_hidden_slice(c + 1, 2 * d + s, half)
+                            if next_c < CHUNKS:
+                                turn_gate_rows(next_c, next_w, 2 * half + s, rows_bank)
+                        if next_c < CHUNKS:
+                            turned_out(next_c, next_w, half, rows_bank)
                         if d == DUOS - 1:
                             close_hidden_sum(c + 1, half)
             if 2 <= j <= rounds + 1:

@@ -17,6 +17,7 @@ STEPS = 8
 FEATURES = 1024
 HIDDEN = 1024
 GATES = 4
+GATE_I, GATE_F, GATE_O, GATE_G = 0, 1, 2, 3
 HALVES = 2
 K_PASS = 4 * P
 PASSES = FEATURES // K_PASS
@@ -46,6 +47,7 @@ def tile_naivelstm_pa_kernel(
     scales_in = [w_ii_scales, w_if__scales, w_io_scales, w_ig_scales]
     hidden_in = [w_hi, w_hf, w_ho, w_hg]
     bias_in = [(b_ii, b_hi), (b_if_, b_hf), (b_io, b_ho), (b_ig, b_hg)]
+    gate_order = [GATE_F, GATE_I, GATE_G, GATE_O]
 
     with ExitStack() as ctx:
         keep = ctx.enter_context(tc.tile_pool(name="keep", bufs=1))
@@ -53,7 +55,8 @@ def tile_naivelstm_pa_kernel(
         turned_pool = ctx.enter_context(tc.tile_pool(name="turned", bufs=6))
         stage = ctx.enter_context(tc.tile_pool(name="stage", bufs=4))
         hidden_pool = ctx.enter_context(tc.tile_pool(name="hidden", bufs=2))
-        gates_pool = ctx.enter_context(tc.tile_pool(name="gates", bufs=6))
+        gates_pool = ctx.enter_context(tc.tile_pool(name="gates", bufs=5))
+        kept_pool = ctx.enter_context(tc.tile_pool(name="kept", bufs=1))
         banks = ctx.enter_context(tc.psum_pool(name="banks", bufs=6))
         hidden_banks = ctx.enter_context(tc.psum_pool(name="hidden_banks", bufs=1))
         ctx.enter_context(tc.manual_schedule())
@@ -63,11 +66,17 @@ def tile_naivelstm_pa_kernel(
         ones = keep.tile([P, P], BF16, name="ones")
         nc.vector.memset(ones[:], 1.0)
         planes = keep.tile([P, GATES, PASSES, HIDDEN], U8, name="planes", align_bytes=64)
-        nc.vector.memset(planes[:].rearrange("p q g n -> p (q g n)").bitcast(I32), 0)
+
+        def zero_planes(q):
+            nc.vector.memset(planes[:, q, :, :].rearrange("p g n -> p (g n)").bitcast(I32), 0)
+
+        zero_planes(gate_order[0])
         bias_rows = keep.tile([P, GATES, HIDDEN], BF16, name="bias_rows")
         nc.vector.memset(bias_rows[:].rearrange("p q n -> p (q n)").bitcast(I32), 0)
+        for q in gate_order[1:]:
+            zero_planes(q)
 
-        for q in range(GATES):
+        for q in gate_order:
             for quad in range(4):
                 nc.gpsimd.dma_start(
                     out=planes[32 * quad : 32 * quad + 4, q, :, :].bitcast(F32),
@@ -79,26 +88,36 @@ def tile_naivelstm_pa_kernel(
 
         hidden_rows = {}
 
+        def load_gate_rows(c, q):
+            rows = rows_pool.tile([P, ROW_TILES, HIDDEN], BF16, name="rows", tag="rows")
+            nc.sync.dma_start(
+                out=rows[:],
+                in_=hidden_in[q][c * CHUNK : (c + 1) * CHUNK, :].rearrange("(a p) k -> p a k", p=P),
+            )
+            hidden_rows[(c, q)] = rows
+
         def load_hidden_rows(c):
             for q in range(GATES):
-                rows = rows_pool.tile([P, ROW_TILES, HIDDEN], BF16, name="rows", tag="rows")
-                nc.sync.dma_start(
-                    out=rows[:],
-                    in_=hidden_in[q][c * CHUNK : (c + 1) * CHUNK, :].rearrange("(a p) k -> p a k", p=P),
-                )
-                hidden_rows[(c, q)] = rows
+                load_gate_rows(c, q)
 
         w_codes = {}
 
+        def load_gate_codes(c, q):
+            codes = keep.tile([P, PASSES, CHUNK], U32, name="w_codes_%d_%d" % (c, q), align_bytes=64)
+            packed = words_in[q].rearrange("g p n t -> p g (n t)")
+            nc.sync.dma_start(
+                out=codes[:].bitcast(I32),
+                in_=packed[:, :, 4 * c * CHUNK : 4 * (c + 1) * CHUNK].bitcast(I32),
+            )
+            w_codes[(c, q)] = codes
+
         def load_codes(c):
-            for q in range(GATES):
-                codes = keep.tile([P, PASSES, CHUNK], U32, name="w_codes_%d_%d" % (c, q), align_bytes=64)
-                packed = words_in[q].rearrange("g p n t -> p g (n t)")
-                nc.sync.dma_start(
-                    out=codes[:].bitcast(I32),
-                    in_=packed[:, :, 4 * c * CHUNK : 4 * (c + 1) * CHUNK].bitcast(I32),
-                )
-                w_codes[(c, q)] = codes
+            for q in gate_order:
+                load_gate_codes(c, q)
+
+        def load_bias(b):
+            q, r = divmod(b, 2)
+            nc.sync.dma_start(out=bias_rows[r : r + 1, q, :], in_=bias_in[q][r].rearrange("n o -> o n"))
 
         x_duos = {}
 
@@ -107,13 +126,21 @@ def tile_naivelstm_pa_kernel(
             nc.sync.dma_start(out=x_duos[d][:], in_=inputs[:, DUO * d : DUO * (d + 1), :])
 
         load_hidden_rows(0)
-        for q in range(GATES):
-            for r in range(2):
-                nc.scalar.dma_start(out=bias_rows[r : r + 1, q, :], in_=bias_in[q][r].rearrange("n o -> o n"))
+        for b in range(0, 3):
+            load_bias(b)
         for d in range(DUOS):
             load_inputs(d)
-        load_hidden_rows(1)
-        load_codes(0)
+        load_gate_codes(0, gate_order[0])
+        for b in range(3, 6):
+            load_bias(b)
+        for q in gate_order[1:]:
+            load_gate_codes(0, q)
+        load_gate_rows(1, 0)
+        load_gate_rows(1, 1)
+        for b in range(6, 8):
+            load_bias(b)
+        load_gate_rows(1, 2)
+        load_gate_rows(1, 3)
         c0_sb = keep.tile([P, HIDDEN], BF16, name="c0_sb")
         nc.sync.dma_start(out=c0_sb[:], in_=c0[0])
         load_codes(1)
@@ -140,16 +167,19 @@ def tile_naivelstm_pa_kernel(
                     ident[:],
                 )
 
-        def turned_out(c, w, half, bank):
+        def turned_out(c, w, half, bank, engine):
             if half == 0:
                 turned[(c, w)] = turned_pool.tile([P, GATES * CHUNK], F32, name="turned", tag="turned")
-            nc.scalar.copy(out=turned[(c, w)][:, half * BANK : (half + 1) * BANK], in_=bank[:])
+            if engine == "scalar":
+                nc.scalar.copy(out=turned[(c, w)][:, half * BANK : (half + 1) * BANK], in_=bank[:])
+            else:
+                nc.vector.tensor_copy(out=turned[(c, w)][:, half * BANK : (half + 1) * BANK], in_=bank[:])
 
-        def turn_hidden_rows(c, w, half):
+        def turn_hidden_rows(c, w, half, engine):
             bank = banks.tile([P, BANK], F32, name="rows_bank", tag="bank")
             for s in range(2):
                 turn_gate_rows(c, w, 2 * half + s, bank)
-            turned_out(c, w, half, bank)
+            turned_out(c, w, half, bank, engine)
 
         hidden_sum = {}
 
@@ -204,54 +234,51 @@ def tile_naivelstm_pa_kernel(
             x_scales[t] = keep.tile([P, PASSES * P], U8, name="x_scales_%d" % t, align_bytes=64)
             nc.vector.quantize_mx(out=x_codes[t][:].bitcast(FP8X4), scales=x_scales[t][:], in_=grouped[:])
 
-        def gate_sums(c, t, hidden_sb, z_sb):
-            for half in range(HALVES):
-                bank = banks.tile([P, BANK], F32, name="z_bank", tag="bank")
-                for s in range(2):
-                    q = 2 * half + s
-                    for g in range(PASSES):
-                        nc.tensor.matmul_mx(
-                            out=bank[:, s * CHUNK : (s + 1) * CHUNK],
-                            lhsT=x_codes[t][:, g * P : (g + 1) * P].bitcast(FP8X4),
-                            lhsT_scale=x_scales[t][:, g * P : (g + 1) * P],
-                            rhs=w_codes[(c, q)][:, g, :].bitcast(FP8X4),
-                            rhs_scale=planes[:, q, g, c * CHUNK : (c + 1) * CHUNK],
-                            start=(g == 0),
-                            stop=(g == PASSES - 1),
-                        )
-                nc.vector.tensor_tensor(
-                    out=z_sb[:, t % DUO, half * BANK : (half + 1) * BANK],
-                    in0=bank[:],
-                    in1=hidden_sb[:, half * BANK : (half + 1) * BANK],
-                    op=ALU.add,
-                )
+        def gate_sums(c, d, q, hidden_sb, z_sb):
+            bank = banks.tile([P, BANK], F32, name="z_bank", tag="bank")
+            for s in range(DUO):
+                t = DUO * d + s
+                for g in range(PASSES):
+                    nc.tensor.matmul_mx(
+                        out=bank[:, s * CHUNK : (s + 1) * CHUNK],
+                        lhsT=x_codes[t][:, g * P : (g + 1) * P].bitcast(FP8X4),
+                        lhsT_scale=x_scales[t][:, g * P : (g + 1) * P],
+                        rhs=w_codes[(c, q)][:, g, :].bitcast(FP8X4),
+                        rhs_scale=planes[:, q, g, c * CHUNK : (c + 1) * CHUNK],
+                        start=(g == 0),
+                        stop=(g == PASSES - 1),
+                    )
+            nc.vector.tensor_tensor(
+                out=z_sb[:, q, :, :],
+                in0=bank[:].rearrange("p (s n) -> p s n", s=DUO),
+                in1=hidden_sb[:, q * CHUNK : (q + 1) * CHUNK].unsqueeze(1).to_broadcast([P, DUO, CHUNK]),
+                op=ALU.add,
+            )
 
-        def gate(z_sb, q):
-            return z_sb[:, :, q * CHUNK : (q + 1) * CHUNK]
+        def activate(z_sb, q):
+            nc.scalar.activation(out=z_sb[:, q, :, :], in_=z_sb[:, q, :, :], func=(ACT.Tanh if q == GATE_G else ACT.Sigmoid))
 
-        def activate(z_sb, first, last, func):
-            gates = z_sb[:, :, first * CHUNK : (last + 1) * CHUNK]
-            nc.scalar.activation(out=gates, in_=gates, func=func)
-
-        def cell_products(c, z_sb):
+        def cell_products(c, z_sb, engine):
             c0_chunk = c0_sb[:, c * CHUNK : (c + 1) * CHUNK].unsqueeze(1).to_broadcast([P, DUO, CHUNK])
-            nc.gpsimd.tensor_tensor(out=gate(z_sb, 1), in0=gate(z_sb, 1), in1=c0_chunk, op=ALU.mult)
-            nc.gpsimd.tensor_tensor(out=gate(z_sb, 0), in0=gate(z_sb, 0), in1=gate(z_sb, 3), op=ALU.mult)
+            kept = kept_pool.tile([P, DUO, CHUNK], F32, name="kept")
+            engine.tensor_tensor(out=kept[:], in0=z_sb[:, GATE_F, :, :], in1=c0_chunk, op=ALU.mult)
+            engine.tensor_tensor(out=z_sb[:, GATE_I, :, :], in0=z_sb[:, GATE_I, :, :], in1=z_sb[:, GATE_G, :, :], op=ALU.mult)
+            return kept
 
-        def cell_state(c, d, z_sb):
+        def cell_state(c, d, z_sb, kept):
             cell = stage.tile([P, DUO, CHUNK], F32, name="cell")
-            nc.vector.tensor_tensor(out=cell[:], in0=gate(z_sb, 1), in1=gate(z_sb, 0), op=ALU.add)
+            nc.vector.tensor_tensor(out=cell[:], in0=kept[:], in1=z_sb[:, GATE_I, :, :], op=ALU.add)
             if d == DUOS - 1:
                 nc.sync.dma_start(out=out_2[0, :, c * CHUNK : (c + 1) * CHUNK], in_=cell[:, DUO - 1, :])
             return cell
 
         def cell_tanh(z_sb, cell):
-            nc.scalar.activation(out=gate(z_sb, 3), in_=cell[:], func=ACT.Tanh)
+            nc.scalar.activation(out=z_sb[:, GATE_G, :, :], in_=cell[:], func=ACT.Tanh)
 
         def hidden_state(c, d, z_sb):
             cols = slice(c * CHUNK, (c + 1) * CHUNK)
             h_sb = stage.tile([P, DUO, CHUNK], F32, name="h_sb")
-            nc.vector.tensor_tensor(out=h_sb[:], in0=gate(z_sb, 2), in1=gate(z_sb, 3), op=ALU.mult)
+            nc.vector.tensor_tensor(out=h_sb[:], in0=z_sb[:, GATE_O, :, :], in1=z_sb[:, GATE_G, :, :], op=ALU.mult)
             nc.sync.dma_start(out=out_0[DUO * d : DUO * (d + 1), :, cols].rearrange("t b n -> b t n"), in_=h_sb[:])
             if d == DUOS - 1:
                 nc.sync.dma_start(out=out_1[0, :, cols], in_=h_sb[:, DUO - 1, :])
@@ -259,7 +286,7 @@ def tile_naivelstm_pa_kernel(
         h0_t = turn_h0()
         for half in range(HALVES):
             for w in range(WORD_TILES):
-                turn_hidden_rows(0, w, half)
+                turn_hidden_rows(0, w, half, "scalar" if w % 2 == 0 else "vector")
         grouped_of = {}
         for half in range(HALVES):
             for k in range(K_SLICES):
@@ -275,27 +302,28 @@ def tile_naivelstm_pa_kernel(
             close_hidden_sum(0, half)
         quantise_inputs(STEPS - 1, grouped_of[STEPS - 1])
         for half in range(HALVES):
-            turn_hidden_rows(1, 0, half)
+            turn_hidden_rows(1, 0, half, "scalar")
 
         rounds = CHUNKS * DUOS
         z_of = {}
+        kept_of = {}
         cell_of = {}
         hidden_sb = None
-        for j in range(rounds + 3):
+        late_copy = None
+        for j in range(rounds + 2):
             c, d = divmod(j, DUOS)
             if 1 <= j <= rounds:
-                activate(z_of[j - 1], 0, 1, ACT.Sigmoid)
-                activate(z_of[j - 1], 3, 3, ACT.Tanh)
-                cell_products((j - 1) // DUOS, z_of[j - 1])
-                activate(z_of[j - 1], 2, 2, ACT.Sigmoid)
-            if j >= 3:
-                cell_tanh(z_of[j - 3], cell_of[j - 3])
+                kept_of[j - 1] = cell_products((j - 1) // DUOS, z_of[j - 1], nc.gpsimd if j < rounds else nc.vector)
+            if late_copy is not None:
+                turned_out(*late_copy)
+                late_copy = None
             if j < rounds:
                 if d == 0:
                     hidden_sb = hidden_sum_out(c)
-                z_of[j] = gates_pool.tile([P, DUO, GATES * CHUNK], F32, name="z_sb", tag="z_sb")
-                for t in range(DUO * d, DUO * (d + 1)):
-                    gate_sums(c, t, hidden_sb, z_of[j])
+                z_of[j] = gates_pool.tile([P, GATES, DUO, CHUNK], F32, name="z_sb", tag="z_sb")
+                for q in gate_order:
+                    gate_sums(c, d, q, hidden_sb, z_of[j])
+                    activate(z_of[j], q)
                 if c + 1 < CHUNKS:
                     next_c, next_w = divmod(j + WORD_TILES + 1, WORD_TILES)
                     for half in range(HALVES):
@@ -306,10 +334,14 @@ def tile_naivelstm_pa_kernel(
                             if next_c < CHUNKS:
                                 turn_gate_rows(next_c, next_w, 2 * half + s, rows_bank)
                         if next_c < CHUNKS:
-                            turned_out(next_c, next_w, half, rows_bank)
+                            if half == 0:
+                                turned_out(next_c, next_w, half, rows_bank, "scalar")
+                            else:
+                                late_copy = (next_c, next_w, half, rows_bank, "scalar")
                         if d == DUOS - 1:
                             close_hidden_sum(c + 1, half)
+            if 1 <= j <= rounds:
+                cell_of[j - 1] = cell_state((j - 1) // DUOS, (j - 1) % DUOS, z_of[j - 1], kept_of[j - 1])
+                cell_tanh(z_of[j - 1], cell_of[j - 1])
             if 2 <= j <= rounds + 1:
-                cell_of[j - 2] = cell_state((j - 2) // DUOS, (j - 2) % DUOS, z_of[j - 2])
-            if j >= 3:
-                hidden_state((j - 3) // DUOS, (j - 3) % DUOS, z_of[j - 3])
+                hidden_state((j - 2) // DUOS, (j - 2) % DUOS, z_of[j - 2])

@@ -30,6 +30,8 @@ K_SLICES = HIDDEN // P
 DUO = 2
 DUOS = STEPS // DUO
 
+WARM_FIRST = 5
+
 FLOPS = 2 * P * STEPS * FEATURES * GATES * HIDDEN + 2 * P * HIDDEN * GATES * HIDDEN
 
 
@@ -63,18 +65,21 @@ def tile_naivelstm_pa_kernel(
 
         ident = keep.tile([P, P], F32, name="ident")
         make_identity(nc, ident[:])
-        ones = keep.tile([P, P], BF16, name="ones")
-        nc.vector.memset(ones[:], 1.0)
         planes = keep.tile([P, GATES, PASSES, HIDDEN], U8, name="planes", align_bytes=64)
 
         def zero_planes(q):
             nc.vector.memset(planes[:, q, :, :].rearrange("p g n -> p (g n)").bitcast(I32), 0)
 
         zero_planes(gate_order[0])
+        ones = keep.tile([P, P], BF16, name="ones")
+        nc.vector.memset(ones[:], 1.0)
+        zeros = keep.tile([P, BANK], BF16, name="zeros")
+        nc.vector.memset(zeros[:], 0.0)
+        zero_planes(gate_order[1])
         bias_rows = keep.tile([P, GATES, HIDDEN], BF16, name="bias_rows")
         nc.vector.memset(bias_rows[:].rearrange("p q n -> p (q n)").bitcast(I32), 0)
-        for q in gate_order[1:]:
-            zero_planes(q)
+        zero_planes(gate_order[2])
+        zero_planes(gate_order[3])
 
         for q in gate_order:
             for quad in range(4):
@@ -88,13 +93,13 @@ def tile_naivelstm_pa_kernel(
 
         hidden_rows = {}
 
-        def load_gate_rows(c, q):
-            rows = rows_pool.tile([P, ROW_TILES, HIDDEN], BF16, name="rows", tag="rows")
+        def load_gate_rows(c, q, first=0, last=HIDDEN):
+            if first == 0:
+                hidden_rows[(c, q)] = rows_pool.tile([P, ROW_TILES, HIDDEN], BF16, name="rows", tag="rows")
             nc.sync.dma_start(
-                out=rows[:],
-                in_=hidden_in[q][c * CHUNK : (c + 1) * CHUNK, :].rearrange("(a p) k -> p a k", p=P),
+                out=hidden_rows[(c, q)][:, :, first:last],
+                in_=hidden_in[q][c * CHUNK : (c + 1) * CHUNK, first:last].rearrange("(a p) k -> p a k", p=P),
             )
-            hidden_rows[(c, q)] = rows
 
         def load_hidden_rows(c):
             for q in range(GATES):
@@ -128,25 +133,28 @@ def tile_naivelstm_pa_kernel(
         load_hidden_rows(0)
         for b in range(0, 3):
             load_bias(b)
-        for d in range(DUOS):
+        for d in range(3):
             load_inputs(d)
-        load_gate_codes(0, gate_order[0])
-        for b in range(3, 6):
+        for b in range(3, 5):
             load_bias(b)
-        for q in gate_order[1:]:
-            load_gate_codes(0, q)
-        load_gate_rows(1, 0)
-        load_gate_rows(1, 1)
-        for b in range(6, 8):
+        load_inputs(3)
+        for q in range(GATES):
+            load_gate_rows(1, q, 0, HIDDEN // 2)
+        for b in range(5, 8):
             load_bias(b)
-        load_gate_rows(1, 2)
-        load_gate_rows(1, 3)
+        load_codes(0)
+        for q in range(GATES):
+            load_gate_rows(1, q, HIDDEN // 2, HIDDEN)
         c0_sb = keep.tile([P, HIDDEN], BF16, name="c0_sb")
         nc.sync.dma_start(out=c0_sb[:], in_=c0[0])
         load_codes(1)
         for c in range(2, CHUNKS):
             load_hidden_rows(c)
             load_codes(c)
+
+        def warm_up():
+            bank = hidden_banks.tile([P, BANK], F32, name="warm_bank", tag="hidden_sum_1")
+            nc.tensor.matmul(out=bank[:], lhsT=ones[:], rhs=zeros[:], start=True, stop=True)
 
         def turn_h0():
             bank = banks.tile([P, BANK], F32, name="h0_bank", tag="bank")
@@ -212,11 +220,20 @@ def tile_naivelstm_pa_kernel(
                 nc.vector.tensor_copy(out=hidden_sb[:, half * BANK : (half + 1) * BANK], in_=hidden_sum[(c, half)][:])
             return hidden_sb
 
+        sorted_duos = {}
+
+        def sort_inputs(d):
+            sorted_duos[d] = keep.tile([P, DUO * FEATURES // 2], F32, name="sorted_%d" % d)
+            nc.vector.tensor_copy(
+                out=sorted_duos[d][:].rearrange("p (a u b) -> p a u b", u=2, b=P),
+                in_=x_duos[d][:].rearrange("p s k -> p (s k)").bitcast(F32).rearrange("p (a b u) -> p a u b", u=2, b=P),
+            )
+
         def turn_inputs(t, g, bank):
-            x_words = x_duos[t // DUO][:, t % DUO, :].bitcast(F32)
             for u in range(2):
                 col = (2 * g + u) * P
-                nc.tensor.transpose(bank[:, col : col + P], x_words[:, 2 * P * g + u : 2 * P * (g + 1) : 2], ident[:])
+                at = ((t % DUO) * PASSES * 2 + 2 * g + u) * P
+                nc.tensor.transpose(bank[:, col : col + P], sorted_duos[t // DUO][:, at : at + P], ident[:])
 
         def group_inputs(bank):
             grouped = stage.tile([P, FEATURES], BF16, name="grouped", align_bytes=64)
@@ -283,23 +300,49 @@ def tile_naivelstm_pa_kernel(
             if d == DUOS - 1:
                 nc.sync.dma_start(out=out_1[0, :, cols], in_=h_sb[:, DUO - 1, :])
 
+        for n in range(WARM_FIRST):
+            warm_up()
         h0_t = turn_h0()
-        for half in range(HALVES):
+        for d in range(DUOS):
+            sort_inputs(d)
+
+        first_banks = {}
+
+        def turn_first(w, q):
+            half = q // 2
+            if q % 2 == 0:
+                first_banks[w] = banks.tile([P, BANK], F32, name="rows_bank", tag="bank")
+            turn_gate_rows(0, w, q, first_banks[w])
+            if q % 2 == 1:
+                turned_out(0, w, half, first_banks[w], "scalar")
+
+        for q in range(2):
             for w in range(WORD_TILES):
-                turn_hidden_rows(0, w, half, "scalar" if w % 2 == 0 else "vector")
+                turn_first(w, q)
+                if w % 2 == 1:
+                    warm_up()
         grouped_of = {}
-        for half in range(HALVES):
-            for k in range(K_SLICES):
-                add_hidden_slice(0, k, half)
-                t, g = divmod(half * K_SLICES + k, PASSES)
-                if g == 0:
-                    x_bank = banks.tile([P, BANK], F32, name="x_bank", tag="bank")
-                turn_inputs(t, g, x_bank)
-                if g == PASSES - 1:
-                    grouped_of[t] = group_inputs(x_bank)
-                    if t > 0:
-                        quantise_inputs(t - 1, grouped_of[t - 1])
-            close_hidden_sum(0, half)
+        x_banks = {}
+
+        def turn_next_inputs(job):
+            t, g = divmod(job, PASSES)
+            if g == 0:
+                x_banks[t] = banks.tile([P, BANK], F32, name="x_bank", tag="bank")
+            turn_inputs(t, g, x_banks[t])
+            if g == PASSES - 1:
+                grouped_of[t] = group_inputs(x_banks[t])
+                if t > 0:
+                    quantise_inputs(t - 1, grouped_of[t - 1])
+
+        for k in range(K_SLICES):
+            add_hidden_slice(0, k, 0)
+            turn_first(k % WORD_TILES, 2 + k // WORD_TILES)
+        for k in range(K_SLICES):
+            add_hidden_slice(0, k, 1)
+            turn_next_inputs(2 * k)
+            turn_next_inputs(2 * k + 1)
+        close_hidden_sum(0, 0)
+        close_hidden_sum(0, 1)
         quantise_inputs(STEPS - 1, grouped_of[STEPS - 1])
         for half in range(HALVES):
             turn_hidden_rows(1, 0, half, "scalar")

@@ -70,23 +70,29 @@ def tile_naivelstm_pa_kernel(
         def zero_planes(q):
             nc.vector.memset(planes[:, q, :, :].rearrange("p g n -> p (g n)").bitcast(I32), 0)
 
-        zero_planes(gate_order[0])
         ones = keep.tile([P, P], BF16, name="ones")
         nc.vector.memset(ones[:], 1.0)
         zeros = keep.tile([P, BANK], BF16, name="zeros")
         nc.vector.memset(zeros[:], 0.0)
-        zero_planes(gate_order[1])
         bias_rows = keep.tile([P, GATES, HIDDEN], BF16, name="bias_rows")
         nc.vector.memset(bias_rows[:].rearrange("p q n -> p (q n)").bitcast(I32), 0)
-        zero_planes(gate_order[2])
-        zero_planes(gate_order[3])
-
         for q in gate_order:
+            zero_planes(q)
+
+        for q in gate_order[:2]:
             for quad in range(4):
                 nc.gpsimd.dma_start(
                     out=planes[32 * quad : 32 * quad + 4, q, :, :].bitcast(F32),
                     in_=scales_in[q][:, 4 * quad : 4 * quad + 4, :].rearrange("g r n -> r g n").bitcast(F32),
                 )
+
+        def load_plane(n):
+            q = gate_order[2 + n // 4]
+            quad = n % 4
+            nc.sync.dma_start(
+                out=planes[32 * quad : 32 * quad + 4, q, :, :].bitcast(I32),
+                in_=scales_in[q][:, 4 * quad : 4 * quad + 4, :].rearrange("g r n -> r g n").bitcast(I32),
+            )
 
         h0_sb = keep.tile([P, HIDDEN], BF16, name="h0_sb")
         nc.sync.dma_start(out=h0_sb[:], in_=h0[0])
@@ -130,18 +136,24 @@ def tile_naivelstm_pa_kernel(
             x_duos[d] = keep.tile([P, DUO, FEATURES], BF16, name="x_duo_%d" % d)
             nc.sync.dma_start(out=x_duos[d][:], in_=inputs[:, DUO * d : DUO * (d + 1), :])
 
-        load_hidden_rows(0)
-        for b in range(0, 3):
+        load_gate_rows(0, 0)
+        load_gate_rows(0, 1)
+        for b in range(0, 5):
             load_bias(b)
-        for d in range(3):
-            load_inputs(d)
-        for b in range(3, 5):
-            load_bias(b)
-        load_inputs(3)
-        for q in range(GATES):
-            load_gate_rows(1, q, 0, HIDDEN // 2)
+        load_gate_rows(0, 2)
+        load_gate_rows(0, 3)
+        load_inputs(0)
         for b in range(5, 8):
             load_bias(b)
+        load_plane(0)
+        load_plane(1)
+        for d in range(1, DUOS):
+            load_inputs(d)
+        for n in range(2, 7):
+            load_plane(n)
+        for q in range(GATES):
+            load_gate_rows(1, q, 0, HIDDEN // 2)
+        load_plane(7)
         load_codes(0)
         for q in range(GATES):
             load_gate_rows(1, q, HIDDEN // 2, HIDDEN)

@@ -54,7 +54,7 @@ def tile_naivelstm_pa_kernel(
     with ExitStack() as ctx:
         keep = ctx.enter_context(tc.tile_pool(name="keep", bufs=1))
         rows_pool = ctx.enter_context(tc.tile_pool(name="rows", bufs=2 * GATES))
-        turned_pool = ctx.enter_context(tc.tile_pool(name="turned", bufs=6))
+        turned_pool = ctx.enter_context(tc.tile_pool(name="turned", bufs=2))
         stage = ctx.enter_context(tc.tile_pool(name="stage", bufs=4))
         hidden_pool = ctx.enter_context(tc.tile_pool(name="hidden", bufs=2))
         gates_pool = ctx.enter_context(tc.tile_pool(name="gates", bufs=5))
@@ -65,6 +65,8 @@ def tile_naivelstm_pa_kernel(
 
         ident = keep.tile([P, P], F32, name="ident")
         make_identity(nc, ident[:])
+        ident_bf = keep.tile([P, P], BF16, name="ident_bf")
+        make_identity(nc, ident_bf[:])
         planes = keep.tile([P, GATES, PASSES, HIDDEN], U8, name="planes", align_bytes=64)
 
         def zero_planes(q):
@@ -169,37 +171,30 @@ def tile_naivelstm_pa_kernel(
             nc.tensor.matmul(out=bank[:], lhsT=ones[:], rhs=zeros[:], start=True, stop=True)
 
         def turn_h0():
-            bank = banks.tile([P, BANK], F32, name="h0_bank", tag="bank")
-            for w in range(WORD_TILES):
-                nc.tensor.transpose(bank[:, w * P : (w + 1) * P], h0_sb[:].bitcast(F32)[:, w * P : (w + 1) * P], ident[:])
-            h0_t = keep.tile([P, WORD_TILES * P], F32, name="h0_t")
+            bank = banks.tile([P, HIDDEN], BF16, name="h0_bank", tag="bank")
+            for k in range(K_SLICES):
+                nc.tensor.transpose(bank[:, k * P : (k + 1) * P], h0_sb[:, k * P : (k + 1) * P], ident_bf[:])
+            h0_t = keep.tile([P, HIDDEN], BF16, name="h0_t")
             nc.vector.tensor_copy(out=h0_t[:], in_=bank[:])
             return h0_t
 
         turned = {}
 
-        def turn_gate_rows(c, w, q, bank):
-            for a in range(ROW_TILES):
-                col = ((q % 2) * ROW_TILES + a) * P
-                nc.tensor.transpose(
-                    bank[:, col : col + P],
-                    hidden_rows[(c, q)][:, a, :].bitcast(F32)[:, w * P : (w + 1) * P],
-                    ident[:],
-                )
+        def new_turned(c):
+            turned[c] = turned_pool.tile([P, K_SLICES, GATES * CHUNK], BF16, name="turned", tag="turned")
 
-        def turned_out(c, w, half, bank, engine):
-            if half == 0:
-                turned[(c, w)] = turned_pool.tile([P, GATES * CHUNK], F32, name="turned", tag="turned")
-            if engine == "scalar":
-                nc.scalar.copy(out=turned[(c, w)][:, half * BANK : (half + 1) * BANK], in_=bank[:])
-            else:
-                nc.vector.tensor_copy(out=turned[(c, w)][:, half * BANK : (half + 1) * BANK], in_=bank[:])
+        def turn_block(c, k, q, a, bank, col):
+            nc.tensor.transpose(bank[:, col : col + P], hidden_rows[(c, q)][:, a, k * P : (k + 1) * P], ident_bf[:])
 
-        def turn_hidden_rows(c, w, half, engine):
-            bank = banks.tile([P, BANK], F32, name="rows_bank", tag="bank")
-            for s in range(2):
-                turn_gate_rows(c, w, 2 * half + s, bank)
-            turned_out(c, w, half, bank, engine)
+        slice_banks = {}
+
+        def turn_slice(c, k, blocks):
+            for n in blocks:
+                if n == 0:
+                    slice_banks[k] = banks.tile([P, GATES * CHUNK], BF16, name="rows_bank", tag="bank")
+                turn_block(c, k, n // ROW_TILES, n % ROW_TILES, slice_banks[k], n * P)
+                if n == GATES * ROW_TILES - 1:
+                    nc.scalar.copy(out=turned[c][:, k, :], in_=slice_banks[k][:])
 
         hidden_sum = {}
 
@@ -213,15 +208,12 @@ def tile_naivelstm_pa_kernel(
             )
 
         def add_hidden_slice(c, k, half):
-            w, e = divmod(k, 2)
             if k == 0:
                 hidden_sum[(c, half)] = hidden_banks.tile([P, BANK], F32, name="hidden_sum_%d" % half)
-            h0_pairs = h0_t[:].bitcast(BF16).rearrange("p (b e) -> p b e", e=2)
-            w_pairs = turned[(c, w)][:].bitcast(BF16).rearrange("p (n e) -> p n e", e=2)
             nc.tensor.matmul(
                 out=hidden_sum[(c, half)][:],
-                lhsT=h0_pairs[:, w * P : (w + 1) * P, e],
-                rhs=w_pairs[:, half * BANK : (half + 1) * BANK, e],
+                lhsT=h0_t[:, k * P : (k + 1) * P],
+                rhs=turned[c][:, k, half * BANK : (half + 1) * BANK],
                 start=(k == 0),
                 stop=False,
             )
@@ -318,20 +310,26 @@ def tile_naivelstm_pa_kernel(
         for d in range(DUOS):
             sort_inputs(d)
 
+        new_turned(0)
         first_banks = {}
+        FOUR = K_SLICES // 2
 
-        def turn_first(w, q):
-            half = q // 2
-            if q % 2 == 0:
-                first_banks[w] = banks.tile([P, BANK], F32, name="rows_bank", tag="bank")
-            turn_gate_rows(0, w, q, first_banks[w])
-            if q % 2 == 1:
-                turned_out(0, w, half, first_banks[w], "scalar")
+        def turn_first(q, k):
+            if k % FOUR == 0:
+                first_banks[q] = banks.tile([P, FOUR, CHUNK], BF16, name="rows_bank", tag="bank")
+            for a in range(ROW_TILES):
+                nc.tensor.transpose(
+                    first_banks[q][:, k % FOUR, a * P : (a + 1) * P],
+                    hidden_rows[(0, q)][:, a, k * P : (k + 1) * P],
+                    ident_bf[:],
+                )
+            if k % FOUR == FOUR - 1:
+                nc.scalar.copy(out=turned[0][:, k - FOUR + 1 : k + 1, q * CHUNK : (q + 1) * CHUNK], in_=first_banks[q][:])
 
         for q in range(2):
-            for w in range(WORD_TILES):
-                turn_first(w, q)
-                if w % 2 == 1:
+            for k in range(K_SLICES):
+                turn_first(q, k)
+                if k % FOUR == FOUR - 1:
                     warm_up()
         grouped_of = {}
         x_banks = {}
@@ -348,7 +346,8 @@ def tile_naivelstm_pa_kernel(
 
         for k in range(K_SLICES):
             add_hidden_slice(0, k, 0)
-            turn_first(k % WORD_TILES, 2 + k // WORD_TILES)
+            turn_first(2 + k // FOUR, 2 * (k % FOUR))
+            turn_first(2 + k // FOUR, 2 * (k % FOUR) + 1)
         for k in range(K_SLICES):
             add_hidden_slice(0, k, 1)
             turn_next_inputs(2 * k)
@@ -356,22 +355,19 @@ def tile_naivelstm_pa_kernel(
         close_hidden_sum(0, 0)
         close_hidden_sum(0, 1)
         quantise_inputs(STEPS - 1, grouped_of[STEPS - 1])
-        for half in range(HALVES):
-            turn_hidden_rows(1, 0, half, "scalar")
+        new_turned(1)
+        for k in range(2):
+            turn_slice(1, k, range(GATES * ROW_TILES))
 
         rounds = CHUNKS * DUOS
         z_of = {}
         kept_of = {}
         cell_of = {}
         hidden_sb = None
-        late_copy = None
         for j in range(rounds + 2):
             c, d = divmod(j, DUOS)
             if 1 <= j <= rounds:
                 kept_of[j - 1] = cell_products((j - 1) // DUOS, z_of[j - 1], nc.gpsimd if j < rounds else nc.vector)
-            if late_copy is not None:
-                turned_out(*late_copy)
-                late_copy = None
             if j < rounds:
                 if d == 0:
                     hidden_sb = hidden_sum_out(c)
@@ -380,21 +376,16 @@ def tile_naivelstm_pa_kernel(
                     gate_sums(c, d, q, hidden_sb, z_of[j])
                     activate(z_of[j], q)
                 if c + 1 < CHUNKS:
-                    next_c, next_w = divmod(j + WORD_TILES + 1, WORD_TILES)
-                    for half in range(HALVES):
+                    next_c, next_d = divmod(j + DUOS + 1, DUOS)
+                    if next_c < CHUNKS and next_d == 0:
+                        new_turned(next_c)
+                    for m in range(4):
+                        add_hidden_slice(c + 1, 2 * d + m % 2, m // 2)
                         if next_c < CHUNKS:
-                            rows_bank = banks.tile([P, BANK], F32, name="rows_bank", tag="bank")
-                        for s in range(2):
-                            add_hidden_slice(c + 1, 2 * d + s, half)
-                            if next_c < CHUNKS:
-                                turn_gate_rows(next_c, next_w, 2 * half + s, rows_bank)
-                        if next_c < CHUNKS:
-                            if half == 0:
-                                turned_out(next_c, next_w, half, rows_bank, "scalar")
-                            else:
-                                late_copy = (next_c, next_w, half, rows_bank, "scalar")
-                        if d == DUOS - 1:
-                            close_hidden_sum(c + 1, half)
+                            turn_slice(next_c, 2 * next_d + m // 2, range(4 * (m % 2), 4 * (m % 2) + 4))
+                    if d == DUOS - 1:
+                        close_hidden_sum(c + 1, 0)
+                        close_hidden_sum(c + 1, 1)
             if 1 <= j <= rounds:
                 cell_of[j - 1] = cell_state((j - 1) // DUOS, (j - 1) % DUOS, z_of[j - 1], kept_of[j - 1])
                 cell_tanh(z_of[j - 1], cell_of[j - 1])

@@ -379,10 +379,12 @@ def tile_naivelstm_pa_kernel(
                     next_c, next_d = divmod(j + DUOS + 1, DUOS)
                     if next_c < CHUNKS and next_d == 0:
                         new_turned(next_c)
+                    blocks = GATES * ROW_TILES
                     for m in range(4):
                         add_hidden_slice(c + 1, 2 * d + m % 2, m // 2)
                         if next_c < CHUNKS:
-                            turn_slice(next_c, 2 * next_d + m // 2, range(4 * (m % 2), 4 * (m % 2) + 4))
+                            for n in range(2 * blocks * m // 3, 2 * blocks * (m + 1) // 3 if m < 3 else 0):
+                                turn_slice(next_c, 2 * next_d + n // blocks, [n % blocks])
                     if d == DUOS - 1:
                         close_hidden_sum(c + 1, 0)
                         close_hidden_sum(c + 1, 1)

@@ -29,6 +29,10 @@ WORD_TILES = HIDDEN // 2 // P
 K_SLICES = HIDDEN // P
 DUO = 2
 DUOS = STEPS // DUO
+LAST = CHUNKS - 1
+HALF_UNITS = CHUNK // 2
+QUAD = 4
+QUADS = STEPS // QUAD
 
 WARM_FIRST = 5
 
@@ -196,6 +200,43 @@ def tile_naivelstm_pa_kernel(
                 if n == GATES * ROW_TILES - 1:
                     nc.scalar.copy(out=turned[c][:, k, :], in_=slice_banks[k][:])
 
+        last_banks = {}
+
+        def turn_last(n):
+            a, rest = divmod(n, K_SLICES * GATES)
+            k, q = divmod(rest, GATES)
+            m = n % (2 * GATES)
+            if m == 0:
+                last_banks[0] = banks.tile([P, GATES * CHUNK], BF16, name="rows_bank", tag="bank")
+            nc.tensor.transpose(last_banks[0][:, m * P : (m + 1) * P], hidden_rows[(LAST, q)][:, a, k * P : (k + 1) * P], ident_bf[:])
+            if m == 2 * GATES - 1:
+                at = (a * K_SLICES + k - 1) * BANK
+                nc.scalar.copy(
+                    out=turned[LAST][:].rearrange("p k n -> p (k n)")[:, at : at + 2 * BANK], in_=last_banks[0][:]
+                )
+
+        def add_last_slice(n):
+            a, k = divmod(n, K_SLICES)
+            if k == 0:
+                hidden_sum[(LAST, a)] = hidden_banks.tile([P, BANK], F32, name="hidden_sum_%d" % a)
+            at = (a * K_SLICES + k) * BANK
+            nc.tensor.matmul(
+                out=hidden_sum[(LAST, a)][:],
+                lhsT=h0_t[:, k * P : (k + 1) * P],
+                rhs=turned[LAST][:].rearrange("p k n -> p (k n)")[:, at : at + BANK],
+                start=(k == 0),
+                stop=False,
+            )
+            if k == K_SLICES - 1:
+                first = LAST * CHUNK + a * HALF_UNITS
+                nc.tensor.matmul(
+                    out=hidden_sum[(LAST, a)][:],
+                    lhsT=ones[:],
+                    rhs=bias_rows[:, :, first : first + HALF_UNITS],
+                    start=False,
+                    stop=True,
+                )
+
         hidden_sum = {}
 
         def close_hidden_sum(c, half):
@@ -219,7 +260,7 @@ def tile_naivelstm_pa_kernel(
             )
 
         def hidden_sum_out(c):
-            hidden_sb = hidden_pool.tile([P, GATES * CHUNK], F32, name="hidden_sb")
+            hidden_sb = hidden_pool.tile([P, GATES * CHUNK], F32, name="hidden_sb", tag="hidden_sb")
             for half in range(HALVES):
                 nc.vector.tensor_copy(out=hidden_sb[:, half * BANK : (half + 1) * BANK], in_=hidden_sum[(c, half)][:])
             return hidden_sb
@@ -255,54 +296,58 @@ def tile_naivelstm_pa_kernel(
             x_scales[t] = keep.tile([P, PASSES * P], U8, name="x_scales_%d" % t, align_bytes=64)
             nc.vector.quantize_mx(out=x_codes[t][:].bitcast(FP8X4), scales=x_scales[t][:], in_=grouped[:])
 
-        def gate_sums(c, d, q, hidden_sb, z_sb):
+        def gate_sums(r, q, hidden_sb, z_sb):
+            first, width, t0, steps = r
+            c, at = divmod(first, CHUNK)
             bank = banks.tile([P, BANK], F32, name="z_bank", tag="bank")
-            for s in range(DUO):
-                t = DUO * d + s
+            for s in range(steps):
                 for g in range(PASSES):
                     nc.tensor.matmul_mx(
-                        out=bank[:, s * CHUNK : (s + 1) * CHUNK],
-                        lhsT=x_codes[t][:, g * P : (g + 1) * P].bitcast(FP8X4),
-                        lhsT_scale=x_scales[t][:, g * P : (g + 1) * P],
-                        rhs=w_codes[(c, q)][:, g, :].bitcast(FP8X4),
-                        rhs_scale=planes[:, q, g, c * CHUNK : (c + 1) * CHUNK],
+                        out=bank[:, s * width : (s + 1) * width],
+                        lhsT=x_codes[t0 + s][:, g * P : (g + 1) * P].bitcast(FP8X4),
+                        lhsT_scale=x_scales[t0 + s][:, g * P : (g + 1) * P],
+                        rhs=w_codes[(c, q)][:, g, at : at + width].bitcast(FP8X4),
+                        rhs_scale=planes[:, q, g, first : first + width],
                         start=(g == 0),
                         stop=(g == PASSES - 1),
                     )
             nc.vector.tensor_tensor(
                 out=z_sb[:, q, :, :],
-                in0=bank[:].rearrange("p (s n) -> p s n", s=DUO),
-                in1=hidden_sb[:, q * CHUNK : (q + 1) * CHUNK].unsqueeze(1).to_broadcast([P, DUO, CHUNK]),
+                in0=bank[:].rearrange("p (s n) -> p s n", s=steps),
+                in1=hidden_sb[:, q * width : (q + 1) * width].unsqueeze(1).to_broadcast([P, steps, width]),
                 op=ALU.add,
             )
 
         def activate(z_sb, q):
             nc.scalar.activation(out=z_sb[:, q, :, :], in_=z_sb[:, q, :, :], func=(ACT.Tanh if q == GATE_G else ACT.Sigmoid))
 
-        def cell_products(c, z_sb, engine):
-            c0_chunk = c0_sb[:, c * CHUNK : (c + 1) * CHUNK].unsqueeze(1).to_broadcast([P, DUO, CHUNK])
-            kept = kept_pool.tile([P, DUO, CHUNK], F32, name="kept")
+        def cell_products(r, z_sb, engine):
+            first, width, t0, steps = r
+            c0_chunk = c0_sb[:, first : first + width].unsqueeze(1).to_broadcast([P, steps, width])
+            kept = kept_pool.tile([P, steps, width], F32, name="kept")
             engine.tensor_tensor(out=kept[:], in0=z_sb[:, GATE_F, :, :], in1=c0_chunk, op=ALU.mult)
             engine.tensor_tensor(out=z_sb[:, GATE_I, :, :], in0=z_sb[:, GATE_I, :, :], in1=z_sb[:, GATE_G, :, :], op=ALU.mult)
             return kept
 
-        def cell_state(c, d, z_sb, kept):
-            cell = stage.tile([P, DUO, CHUNK], F32, name="cell")
+        def cell_state(r, z_sb, kept):
+            first, width, t0, steps = r
+            cell = stage.tile([P, steps, width], F32, name="cell")
             nc.vector.tensor_tensor(out=cell[:], in0=kept[:], in1=z_sb[:, GATE_I, :, :], op=ALU.add)
-            if d == DUOS - 1:
-                nc.sync.dma_start(out=out_2[0, :, c * CHUNK : (c + 1) * CHUNK], in_=cell[:, DUO - 1, :])
+            if t0 + steps == STEPS:
+                nc.sync.dma_start(out=out_2[0, :, first : first + width], in_=cell[:, steps - 1, :])
             return cell
 
         def cell_tanh(z_sb, cell):
             nc.scalar.activation(out=z_sb[:, GATE_G, :, :], in_=cell[:], func=ACT.Tanh)
 
-        def hidden_state(c, d, z_sb):
-            cols = slice(c * CHUNK, (c + 1) * CHUNK)
-            h_sb = stage.tile([P, DUO, CHUNK], F32, name="h_sb")
+        def hidden_state(r, z_sb):
+            first, width, t0, steps = r
+            cols = slice(first, first + width)
+            h_sb = stage.tile([P, steps, width], F32, name="h_sb")
             nc.vector.tensor_tensor(out=h_sb[:], in0=z_sb[:, GATE_O, :, :], in1=z_sb[:, GATE_G, :, :], op=ALU.mult)
-            nc.sync.dma_start(out=out_0[DUO * d : DUO * (d + 1), :, cols].rearrange("t b n -> b t n"), in_=h_sb[:])
-            if d == DUOS - 1:
-                nc.sync.dma_start(out=out_1[0, :, cols], in_=h_sb[:, DUO - 1, :])
+            nc.sync.dma_start(out=out_0[t0 : t0 + steps, :, cols].rearrange("t b n -> b t n"), in_=h_sb[:])
+            if t0 + steps == STEPS:
+                nc.sync.dma_start(out=out_1[0, :, cols], in_=h_sb[:, steps - 1, :])
 
         for n in range(WARM_FIRST):
             warm_up()
@@ -359,37 +404,78 @@ def tile_naivelstm_pa_kernel(
         for k in range(2):
             turn_slice(1, k, range(GATES * ROW_TILES))
 
-        rounds = CHUNKS * DUOS
+        rounds = [(c * CHUNK, CHUNK, DUO * d, DUO) for c in range(LAST) for d in range(DUOS)]
+        rounds += [
+            (LAST * CHUNK + a * HALF_UNITS, HALF_UNITS, QUAD * d, QUAD) for a in range(HALVES) for d in range(QUADS)
+        ]
+        count = len(rounds)
         z_of = {}
         kept_of = {}
         cell_of = {}
         hidden_sb = None
-        for j in range(rounds + 2):
+        blocks = GATES * ROW_TILES
+        last_jobs = {
+            7: ([], range(0, 8)),
+            8: (range(0, 2), range(8, 16)),
+            9: (range(2, 4), range(16, 32)),
+            10: (range(4, 8), range(32, 40)),
+            11: (range(8, 10), range(40, 48)),
+            12: (range(10, 12), range(48, 64)),
+            13: (range(12, 16), range(0)),
+        }
+
+        def prepare(j):
             c, d = divmod(j, DUOS)
-            if 1 <= j <= rounds:
-                kept_of[j - 1] = cell_products((j - 1) // DUOS, z_of[j - 1], nc.gpsimd if j < rounds else nc.vector)
-            if j < rounds:
-                if d == 0:
-                    hidden_sb = hidden_sum_out(c)
-                z_of[j] = gates_pool.tile([P, GATES, DUO, CHUNK], F32, name="z_sb", tag="z_sb")
-                for q in gate_order:
-                    gate_sums(c, d, q, hidden_sb, z_of[j])
-                    activate(z_of[j], q)
-                if c + 1 < CHUNKS:
-                    next_c, next_d = divmod(j + DUOS + 1, DUOS)
-                    if next_c < CHUNKS and next_d == 0:
-                        new_turned(next_c)
-                    blocks = GATES * ROW_TILES
-                    for m in range(4):
-                        add_hidden_slice(c + 1, 2 * d + m % 2, m // 2)
-                        if next_c < CHUNKS:
-                            for n in range(2 * blocks * m // 3, 2 * blocks * (m + 1) // 3 if m < 3 else 0):
-                                turn_slice(next_c, 2 * next_d + n // blocks, [n % blocks])
-                    if d == DUOS - 1:
-                        close_hidden_sum(c + 1, 0)
-                        close_hidden_sum(c + 1, 1)
-            if 1 <= j <= rounds:
-                cell_of[j - 1] = cell_state((j - 1) // DUOS, (j - 1) % DUOS, z_of[j - 1], kept_of[j - 1])
+            adds = []
+            turns = []
+            if c + 1 < LAST:
+                adds = [lambda k=2 * d + m % 2, half=m // 2: add_hidden_slice(c + 1, k, half) for m in range(4)]
+            next_c, next_d = divmod(j + DUOS + 1, DUOS)
+            if next_c < LAST:
+                if next_d == 0:
+                    new_turned(next_c)
+                turns = [lambda n=n: turn_slice(next_c, 2 * next_d + n // blocks, [n % blocks]) for n in range(2 * blocks)]
+            if j in last_jobs:
+                if j == 7:
+                    new_turned(LAST)
+                adds += [lambda n=n: add_last_slice(n) for n in last_jobs[j][0]]
+                turns += [lambda n=n: turn_last(n) for n in last_jobs[j][1]]
+            gaps = len(adds) - 1
+            for m in range(len(adds)):
+                adds[m]()
+                if m < gaps:
+                    for turn in turns[len(turns) * m // gaps : len(turns) * (m + 1) // gaps]:
+                        turn()
+            if c + 1 < LAST and d == DUOS - 1:
+                close_hidden_sum(c + 1, 0)
+                close_hidden_sum(c + 1, 1)
+
+        def half_sum_out(a):
+            half_sb = hidden_pool.tile([P, GATES * CHUNK], F32, name="hidden_sb", tag="hidden_sb")
+            nc.vector.tensor_copy(out=half_sb[:, 0:BANK], in_=hidden_sum[(LAST, a)][:])
+            return half_sb
+
+        for j in range(count):
+            c = rounds[j][0] // CHUNK
+            if j >= 1:
+                kept_of[j - 1] = cell_products(rounds[j - 1], z_of[j - 1], nc.gpsimd)
+            if rounds[j][2] == 0:
+                hidden_sb = hidden_sum_out(c) if c < LAST else half_sum_out(rounds[j][0] % CHUNK // HALF_UNITS)
+            z_of[j] = gates_pool.tile([P, GATES, rounds[j][3], rounds[j][1]], F32, name="z_sb", tag="z_sb")
+            for q in gate_order:
+                gate_sums(rounds[j], q, hidden_sb, z_of[j])
+                activate(z_of[j], q)
+            prepare(j)
+            if j >= 1:
+                cell_of[j - 1] = cell_state(rounds[j - 1], z_of[j - 1], kept_of[j - 1])
                 cell_tanh(z_of[j - 1], cell_of[j - 1])
-            if 2 <= j <= rounds + 1:
-                hidden_state((j - 2) // DUOS, (j - 2) % DUOS, z_of[j - 2])
+            if 2 <= j < count - 1:
+                hidden_state(rounds[j - 2], z_of[j - 2])
+
+        last = count - 1
+        kept_of[last] = cell_products(rounds[last], z_of[last], nc.vector)
+        hidden_state(rounds[last - 2], z_of[last - 2])
+        cell_of[last] = cell_state(rounds[last], z_of[last], kept_of[last])
+        cell_tanh(z_of[last], cell_of[last])
+        hidden_state(rounds[last - 1], z_of[last - 1])
+        hidden_state(rounds[last], z_of[last])

@@ -17,7 +17,7 @@ STEPS = 8
 FEATURES = 1024
 HIDDEN = 1024
 GATES = 4
-GATE_I, GATE_F, GATE_O, GATE_G = 0, 1, 2, 3
+GATE_F, GATE_I, GATE_G, GATE_O = 0, 1, 2, 3
 HALVES = 2
 K_PASS = 4 * P
 PASSES = FEATURES // K_PASS
@@ -49,10 +49,10 @@ def tile_naivelstm_pa_kernel(
     out_0, out_1, out_2,
 ):
     nc = tc.nc
-    words_in = [w_ii_words, w_if__words, w_io_words, w_ig_words]
-    scales_in = [w_ii_scales, w_if__scales, w_io_scales, w_ig_scales]
-    hidden_in = [w_hi, w_hf, w_ho, w_hg]
-    bias_in = [(b_ii, b_hi), (b_if_, b_hf), (b_io, b_ho), (b_ig, b_hg)]
+    words_in = [w_if__words, w_ii_words, w_ig_words, w_io_words]
+    scales_in = [w_if__scales, w_ii_scales, w_ig_scales, w_io_scales]
+    hidden_in = [w_hf, w_hi, w_hg, w_ho]
+    bias_in = [(b_if_, b_hf), (b_ii, b_hi), (b_ig, b_hg), (b_io, b_ho)]
     gate_order = [GATE_F, GATE_I, GATE_G, GATE_O]
 
     with ExitStack() as ctx:
@@ -128,6 +128,19 @@ def tile_naivelstm_pa_kernel(
             )
             w_codes[(c, q)] = codes
 
+        last_codes = {}
+
+        def load_last_codes(a):
+            first = LAST * CHUNK + a * HALF_UNITS
+            for pair in range(2):
+                last_codes[(a, pair)] = keep.tile([P, PASSES, CHUNK], U32, name="last_codes_%d_%d" % (a, pair), align_bytes=64)
+                for r in range(2):
+                    packed = words_in[2 * pair + r].rearrange("g p n t -> p g (n t)")
+                    nc.sync.dma_start(
+                        out=last_codes[(a, pair)][:, :, r * HALF_UNITS : (r + 1) * HALF_UNITS].bitcast(I32),
+                        in_=packed[:, :, 4 * first : 4 * (first + HALF_UNITS)].bitcast(I32),
+                    )
+
         def load_codes(c):
             for q in gate_order:
                 load_gate_codes(c, q)
@@ -166,9 +179,11 @@ def tile_naivelstm_pa_kernel(
         c0_sb = keep.tile([P, HIDDEN], BF16, name="c0_sb")
         nc.sync.dma_start(out=c0_sb[:], in_=c0[0])
         load_codes(1)
-        for c in range(2, CHUNKS):
-            load_hidden_rows(c)
-            load_codes(c)
+        load_hidden_rows(2)
+        load_codes(2)
+        load_hidden_rows(LAST)
+        for a in range(HALVES):
+            load_last_codes(a)
 
         def warm_up():
             bank = hidden_banks.tile([P, BANK], F32, name="warm_bank", tag="hidden_sum_1")
@@ -208,26 +223,27 @@ def tile_naivelstm_pa_kernel(
             m = n % (2 * GATES)
             if m == 0:
                 last_banks[0] = banks.tile([P, GATES * CHUNK], BF16, name="rows_bank", tag="bank")
-            nc.tensor.transpose(last_banks[0][:, m * P : (m + 1) * P], hidden_rows[(LAST, q)][:, a, k * P : (k + 1) * P], ident_bf[:])
+            rows = hidden_rows[(LAST, q)]
+            nc.tensor.transpose(last_banks[0][:, m * P : (m + 1) * P], rows[:, a, k * P : (k + 1) * P], ident_bf[:])
             if m == 2 * GATES - 1:
                 at = (a * K_SLICES + k - 1) * BANK
                 nc.scalar.copy(
                     out=turned[LAST][:].rearrange("p k n -> p (k n)")[:, at : at + 2 * BANK], in_=last_banks[0][:]
                 )
 
-        def add_last_slice(n):
+        def add_last_piece(n, r):
             a, k = divmod(n, K_SLICES)
-            if k == 0:
+            if k == 0 and r == 0:
                 hidden_sum[(LAST, a)] = hidden_banks.tile([P, BANK], F32, name="hidden_sum_%d" % a)
-            at = (a * K_SLICES + k) * BANK
+            at = (a * K_SLICES + k) * BANK + r * CHUNK
             nc.tensor.matmul(
-                out=hidden_sum[(LAST, a)][:],
+                out=hidden_sum[(LAST, a)][:, r * CHUNK : (r + 1) * CHUNK],
                 lhsT=h0_t[:, k * P : (k + 1) * P],
-                rhs=turned[LAST][:].rearrange("p k n -> p (k n)")[:, at : at + BANK],
-                start=(k == 0),
+                rhs=turned[LAST][:].rearrange("p k n -> p (k n)")[:, at : at + CHUNK],
+                start=(k == 0 and r == 0),
                 stop=False,
             )
-            if k == K_SLICES - 1:
+            if k == K_SLICES - 1 and r == 1:
                 first = LAST * CHUNK + a * HALF_UNITS
                 nc.tensor.matmul(
                     out=hidden_sum[(LAST, a)][:],
@@ -318,6 +334,44 @@ def tile_naivelstm_pa_kernel(
                 op=ALU.add,
             )
 
+        last_planes = {}
+
+        def place_last_planes(a):
+            first = LAST * CHUNK + a * HALF_UNITS
+            for pair in range(2):
+                last_planes[(a, pair)] = keep.tile([P, PASSES, CHUNK], U8, name="last_planes_%d_%d" % (a, pair), align_bytes=64)
+                for r in range(2):
+                    nc.vector.tensor_copy(
+                        out=last_planes[(a, pair)][:, :, r * HALF_UNITS : (r + 1) * HALF_UNITS].bitcast(I32),
+                        in_=planes[:, 2 * pair + r, :, first : first + HALF_UNITS].bitcast(I32),
+                    )
+
+        def pair_sums(a, t0, pair, hidden_sb, z_out):
+            bank = banks.tile([P, BANK], F32, name="z_bank", tag="bank")
+            for s in range(DUO):
+                for g in range(PASSES):
+                    nc.tensor.matmul_mx(
+                        out=bank[:, s * CHUNK : (s + 1) * CHUNK],
+                        lhsT=x_codes[t0 + s][:, g * P : (g + 1) * P].bitcast(FP8X4),
+                        lhsT_scale=x_scales[t0 + s][:, g * P : (g + 1) * P],
+                        rhs=last_codes[(a, pair)][:, g, :].bitcast(FP8X4),
+                        rhs_scale=last_planes[(a, pair)][:, g, :],
+                        start=(g == 0),
+                        stop=(g == PASSES - 1),
+                    )
+            nc.vector.tensor_tensor(
+                out=z_out,
+                in0=bank[:].rearrange("p (s n) -> p s n", s=DUO),
+                in1=hidden_sb[:, pair * CHUNK : (pair + 1) * CHUNK].unsqueeze(1).to_broadcast([P, DUO, CHUNK]),
+                op=ALU.add,
+            )
+
+        def gate_of(z_sb, q, width):
+            if width == CHUNK:
+                return z_sb[:, q, :, :]
+            pair, r = divmod(q, 2)
+            return z_sb[:, pair, :, r * HALF_UNITS : (r + 1) * HALF_UNITS]
+
         def activate(z_sb, q):
             nc.scalar.activation(out=z_sb[:, q, :, :], in_=z_sb[:, q, :, :], func=(ACT.Tanh if q == GATE_G else ACT.Sigmoid))
 
@@ -325,26 +379,27 @@ def tile_naivelstm_pa_kernel(
             first, width, t0, steps = r
             c0_chunk = c0_sb[:, first : first + width].unsqueeze(1).to_broadcast([P, steps, width])
             kept = kept_pool.tile([P, steps, width], F32, name="kept")
-            engine.tensor_tensor(out=kept[:], in0=z_sb[:, GATE_F, :, :], in1=c0_chunk, op=ALU.mult)
-            engine.tensor_tensor(out=z_sb[:, GATE_I, :, :], in0=z_sb[:, GATE_I, :, :], in1=z_sb[:, GATE_G, :, :], op=ALU.mult)
+            i_gate = gate_of(z_sb, GATE_I, width)
+            engine.tensor_tensor(out=kept[:], in0=gate_of(z_sb, GATE_F, width), in1=c0_chunk, op=ALU.mult)
+            engine.tensor_tensor(out=i_gate, in0=i_gate, in1=gate_of(z_sb, GATE_G, width), op=ALU.mult)
             return kept
 
         def cell_state(r, z_sb, kept):
             first, width, t0, steps = r
             cell = stage.tile([P, steps, width], F32, name="cell")
-            nc.vector.tensor_tensor(out=cell[:], in0=kept[:], in1=z_sb[:, GATE_I, :, :], op=ALU.add)
+            nc.vector.tensor_tensor(out=cell[:], in0=kept, in1=gate_of(z_sb, GATE_I, width), op=ALU.add)
             if t0 + steps == STEPS:
                 nc.sync.dma_start(out=out_2[0, :, first : first + width], in_=cell[:, steps - 1, :])
             return cell
 
-        def cell_tanh(z_sb, cell):
-            nc.scalar.activation(out=z_sb[:, GATE_G, :, :], in_=cell[:], func=ACT.Tanh)
+        def cell_tanh(r, z_sb, cell):
+            nc.scalar.activation(out=gate_of(z_sb, GATE_G, r[1]), in_=cell[:], func=ACT.Tanh)
 
         def hidden_state(r, z_sb):
             first, width, t0, steps = r
             cols = slice(first, first + width)
             h_sb = stage.tile([P, steps, width], F32, name="h_sb")
-            nc.vector.tensor_tensor(out=h_sb[:], in0=z_sb[:, GATE_O, :, :], in1=z_sb[:, GATE_G, :, :], op=ALU.mult)
+            nc.vector.tensor_tensor(out=h_sb[:], in0=gate_of(z_sb, GATE_O, width), in1=gate_of(z_sb, GATE_G, width), op=ALU.mult)
             nc.sync.dma_start(out=out_0[t0 : t0 + steps, :, cols].rearrange("t b n -> b t n"), in_=h_sb[:])
             if t0 + steps == STEPS:
                 nc.sync.dma_start(out=out_1[0, :, cols], in_=h_sb[:, steps - 1, :])
@@ -419,8 +474,8 @@ def tile_naivelstm_pa_kernel(
             8: (range(0, 2), range(8, 16)),
             9: (range(2, 4), range(16, 32)),
             10: (range(4, 8), range(32, 40)),
-            11: (range(8, 10), range(40, 48)),
-            12: (range(10, 12), range(48, 64)),
+            11: (range(8, 10), range(40, 56)),
+            12: (range(10, 12), range(56, 64)),
             13: (range(12, 16), range(0)),
         }
 
@@ -438,7 +493,7 @@ def tile_naivelstm_pa_kernel(
             if j in last_jobs:
                 if j == 7:
                     new_turned(LAST)
-                adds += [lambda n=n: add_last_slice(n) for n in last_jobs[j][0]]
+                adds += [lambda n=n, r=r: add_last_piece(n, r) for n in last_jobs[j][0] for r in range(2)]
                 turns += [lambda n=n: turn_last(n) for n in last_jobs[j][1]]
             gaps = len(adds) - 1
             for m in range(len(adds)):
@@ -450,32 +505,61 @@ def tile_naivelstm_pa_kernel(
                 close_hidden_sum(c + 1, 0)
                 close_hidden_sum(c + 1, 1)
 
-        def half_sum_out(a):
-            half_sb = hidden_pool.tile([P, GATES * CHUNK], F32, name="hidden_sb", tag="hidden_sb")
-            nc.vector.tensor_copy(out=half_sb[:, 0:BANK], in_=hidden_sum[(LAST, a)][:])
-            return half_sb
+        half_sums = {}
 
+        def half_sum_out(a, copy):
+            half_sums[a] = hidden_pool.tile([P, GATES * CHUNK], F32, name="hidden_sb", tag="hidden_sb")
+            copy(out=half_sums[a][:, 0:BANK], in_=hidden_sum[(LAST, a)][:])
+
+        for a in range(HALVES):
+            place_last_planes(a)
         for j in range(count):
             c = rounds[j][0] // CHUNK
             if j >= 1:
                 kept_of[j - 1] = cell_products(rounds[j - 1], z_of[j - 1], nc.gpsimd)
             if rounds[j][2] == 0:
-                hidden_sb = hidden_sum_out(c) if c < LAST else half_sum_out(rounds[j][0] % CHUNK // HALF_UNITS)
-            z_of[j] = gates_pool.tile([P, GATES, rounds[j][3], rounds[j][1]], F32, name="z_sb", tag="z_sb")
-            for q in gate_order:
-                gate_sums(rounds[j], q, hidden_sb, z_of[j])
-                activate(z_of[j], q)
+                if c < LAST:
+                    hidden_sb = hidden_sum_out(c)
+                else:
+                    if j == count - QUADS:
+                        half_sum_out(1, nc.vector.tensor_copy)
+                    hidden_sb = half_sums[rounds[j][0] % CHUNK // HALF_UNITS]
+            if c < LAST:
+                z_of[j] = gates_pool.tile([P, GATES, DUO, CHUNK], F32, name="z_sb", tag="z_sb")
+                for q in gate_order:
+                    gate_sums(rounds[j], q, hidden_sb, z_of[j])
+                    activate(z_of[j], q)
+            else:
+                z_of[j] = gates_pool.tile([P, 2, QUAD, CHUNK], F32, name="z_sb", tag="z_sb")
+                a = rounds[j][0] % CHUNK // HALF_UNITS
+                for s in range(0, QUAD, DUO):
+                    pair_sums(a, rounds[j][2] + s, 0, hidden_sb, z_of[j][:, 0, s : s + DUO, :])
+                    pair = z_of[j][:, 0, s : s + DUO, :]
+                    nc.scalar.activation(out=pair, in_=pair, func=ACT.Sigmoid)
+                for s in range(0, QUAD, DUO):
+                    pair_sums(a, rounds[j][2] + s, 1, hidden_sb, z_of[j][:, 1, s : s + DUO, :])
+                for q in (GATE_G, GATE_O):
+                    gate = gate_of(z_of[j], q, HALF_UNITS)
+                    nc.scalar.activation(out=gate, in_=gate, func=(ACT.Tanh if q == GATE_G else ACT.Sigmoid))
+            if j == LAST * DUOS - 1:
+                half_sum_out(0, nc.scalar.copy)
             prepare(j)
             if j >= 1:
-                cell_of[j - 1] = cell_state(rounds[j - 1], z_of[j - 1], kept_of[j - 1])
-                cell_tanh(z_of[j - 1], cell_of[j - 1])
-            if 2 <= j < count - 1:
+                cell_of[j - 1] = cell_state(rounds[j - 1], z_of[j - 1], kept_of[j - 1][:])
+                cell_tanh(rounds[j - 1], z_of[j - 1], cell_of[j - 1])
+            if j >= 2:
                 hidden_state(rounds[j - 2], z_of[j - 2])
 
         last = count - 1
         kept_of[last] = cell_products(rounds[last], z_of[last], nc.vector)
-        hidden_state(rounds[last - 2], z_of[last - 2])
-        cell_of[last] = cell_state(rounds[last], z_of[last], kept_of[last])
-        cell_tanh(z_of[last], cell_of[last])
+        first, width, t0, steps = rounds[last]
+        parts = []
+        for s in range(0, QUAD, DUO):
+            part = (first, width, t0 + s, DUO)
+            z_part = z_of[last][:, :, s : s + DUO, :]
+            cell = cell_state(part, z_part, kept_of[last][:, s : s + DUO, :])
+            cell_tanh(part, z_part, cell)
+            parts.append((part, z_part))
         hidden_state(rounds[last - 1], z_of[last - 1])
-        hidden_state(rounds[last], z_of[last])
+        for part, z_part in parts:
+            hidden_state(part, z_part)

@@ -32,6 +32,9 @@ DUOS = STEPS // DUO
 LAST = CHUNKS - 1
 HALF_UNITS = CHUNK // 2
 QUAD = 4
+PLANES_AT = 192
+X_CODES_AT = 16
+X_SCALES_AT = 128
 QUADS = STEPS // QUAD
 
 WARM_FIRST = 5
@@ -61,7 +64,7 @@ def tile_naivelstm_pa_kernel(
         turned_pool = ctx.enter_context(tc.tile_pool(name="turned", bufs=2))
         stage = ctx.enter_context(tc.tile_pool(name="stage", bufs=4))
         hidden_pool = ctx.enter_context(tc.tile_pool(name="hidden", bufs=2))
-        gates_pool = ctx.enter_context(tc.tile_pool(name="gates", bufs=5))
+        gates_pool = ctx.enter_context(tc.tile_pool(name="gates", bufs=4))
         kept_pool = ctx.enter_context(tc.tile_pool(name="kept", bufs=1))
         banks = ctx.enter_context(tc.psum_pool(name="banks", bufs=6))
         hidden_banks = ctx.enter_context(tc.psum_pool(name="hidden_banks", bufs=1))
@@ -71,10 +74,12 @@ def tile_naivelstm_pa_kernel(
         make_identity(nc, ident[:])
         ident_bf = keep.tile([P, P], BF16, name="ident_bf")
         make_identity(nc, ident_bf[:])
-        planes = keep.tile([P, GATES, PASSES, HIDDEN], U8, name="planes", align_bytes=64)
+        planes_flat = keep.tile([P, PLANES_AT + GATES * PASSES * HIDDEN], U8, name="planes", align_bytes=256)
+        planes = planes_flat[:, PLANES_AT:].rearrange("p (q g n) -> p q g n", q=GATES, g=PASSES)
 
         def zero_planes(q):
-            nc.vector.memset(planes[:, q, :, :].rearrange("p g n -> p (g n)").bitcast(I32), 0)
+            at = PLANES_AT + q * PASSES * HIDDEN
+            nc.vector.memset(planes_flat[:, at : at + PASSES * HIDDEN].bitcast(I32), 0)
 
         ones = keep.tile([P, P], BF16, name="ones")
         nc.vector.memset(ones[:], 1.0)
@@ -120,7 +125,7 @@ def tile_naivelstm_pa_kernel(
         w_codes = {}
 
         def load_gate_codes(c, q):
-            codes = keep.tile([P, PASSES, CHUNK], U32, name="w_codes_%d_%d" % (c, q), align_bytes=64)
+            codes = keep.tile([P, PASSES, CHUNK], U32, name="w_codes_%d_%d" % (c, q), align_bytes=256)
             packed = words_in[q].rearrange("g p n t -> p g (n t)")
             nc.sync.dma_start(
                 out=codes[:].bitcast(I32),
@@ -133,7 +138,7 @@ def tile_naivelstm_pa_kernel(
         def load_last_codes(a):
             first = LAST * CHUNK + a * HALF_UNITS
             for pair in range(2):
-                last_codes[(a, pair)] = keep.tile([P, PASSES, CHUNK], U32, name="last_codes_%d_%d" % (a, pair), align_bytes=64)
+                last_codes[(a, pair)] = keep.tile([P, PASSES, CHUNK], U32, name="last_codes_%d_%d" % (a, pair), align_bytes=256)
                 for r in range(2):
                     packed = words_in[2 * pair + r].rearrange("g p n t -> p g (n t)")
                     nc.sync.dma_start(
@@ -308,9 +313,11 @@ def tile_naivelstm_pa_kernel(
         x_scales = {}
 
         def quantise_inputs(t, grouped):
-            x_codes[t] = keep.tile([P, PASSES * P], U32, name="x_codes_%d" % t, align_bytes=64)
-            x_scales[t] = keep.tile([P, PASSES * P], U8, name="x_scales_%d" % t, align_bytes=64)
-            nc.vector.quantize_mx(out=x_codes[t][:].bitcast(FP8X4), scales=x_scales[t][:], in_=grouped[:])
+            codes = keep.tile([P, X_CODES_AT + PASSES * P], U32, name="x_codes_%d" % t, align_bytes=256)
+            scales = keep.tile([P, X_SCALES_AT + PASSES * P], U8, name="x_scales_%d" % t, align_bytes=256)
+            x_codes[t] = codes[:, X_CODES_AT:]
+            x_scales[t] = scales[:, X_SCALES_AT:]
+            nc.vector.quantize_mx(out=x_codes[t].bitcast(FP8X4), scales=x_scales[t], in_=grouped[:])
 
         def gate_sums(r, q, hidden_sb, z_sb):
             first, width, t0, steps = r
@@ -339,7 +346,8 @@ def tile_naivelstm_pa_kernel(
         def place_last_planes(a):
             first = LAST * CHUNK + a * HALF_UNITS
             for pair in range(2):
-                last_planes[(a, pair)] = keep.tile([P, PASSES, CHUNK], U8, name="last_planes_%d_%d" % (a, pair), align_bytes=64)
+                flat = keep.tile([P, PLANES_AT + PASSES * CHUNK], U8, name="last_planes_%d_%d" % (a, pair), align_bytes=256)
+                last_planes[(a, pair)] = flat[:, PLANES_AT:].rearrange("p (g n) -> p g n", g=PASSES)
                 for r in range(2):
                     nc.vector.tensor_copy(
                         out=last_planes[(a, pair)][:, :, r * HALF_UNITS : (r + 1) * HALF_UNITS].bitcast(I32),
@@ -386,7 +394,7 @@ def tile_naivelstm_pa_kernel(
 
         def cell_state(r, z_sb, kept):
             first, width, t0, steps = r
-            cell = stage.tile([P, steps, width], F32, name="cell")
+            cell = stage.tile([P, steps, width], F32, name="cell", bufs=2)
             nc.vector.tensor_tensor(out=cell[:], in0=kept, in1=gate_of(z_sb, GATE_I, width), op=ALU.add)
             if t0 + steps == STEPS:
                 nc.sync.dma_start(out=out_2[0, :, first : first + width], in_=cell[:, steps - 1, :])

from contextlib import ExitStack

import concourse.mybir as mybir
from concourse.masks import make_identity

F32 = mybir.dt.float32
BF16 = mybir.dt.bfloat16
I32 = mybir.dt.int32
U32 = mybir.dt.uint32
U8 = mybir.dt.uint8
FP8X4 = mybir.dt.float8_e4m3fn_x4
ACT = mybir.ActivationFunctionType
ALU = mybir.AluOpType

P = 128
STEPS = 8
FEATURES = 1024
HIDDEN = 1024
GATES = 4
GATE_F, GATE_I, GATE_G, GATE_O = 0, 1, 2, 3
HALVES = 2
K_PASS = 4 * P
PASSES = FEATURES // K_PASS
CHUNK = 256
CHUNKS = HIDDEN // CHUNK
ROW_TILES = CHUNK // P
BANK = 512
WORD_TILES = HIDDEN // 2 // P
K_SLICES = HIDDEN // P
DUO = 2
DUOS = STEPS // DUO
LAST = CHUNKS - 1
HALF_UNITS = CHUNK // 2
QUAD = 4
PLANES_AT = 192
X_CODES_AT = 16
X_SCALES_AT = 128
QUADS = STEPS // QUAD

WARM_FIRST = 5

FLOPS = 2 * P * STEPS * FEATURES * GATES * HIDDEN + 2 * P * HIDDEN * GATES * HIDDEN


def tile_naivelstm_pa_kernel(
    tc,
    inputs, h0, c0,
    w_ii_words, w_ii_scales, b_ii, w_hi, b_hi,
    w_if__words, w_if__scales, b_if_, w_hf, b_hf,
    w_io_words, w_io_scales, b_io, w_ho, b_ho,
    w_ig_words, w_ig_scales, b_ig, w_hg, b_hg,
    out_0, out_1, out_2,
):
    nc = tc.nc
    words_in = [w_if__words, w_ii_words, w_ig_words, w_io_words]
    scales_in = [w_if__scales, w_ii_scales, w_ig_scales, w_io_scales]
    hidden_in = [w_hf, w_hi, w_hg, w_ho]
    bias_in = [(b_if_, b_hf), (b_ii, b_hi), (b_ig, b_hg), (b_io, b_ho)]
    gate_order = [GATE_F, GATE_I, GATE_G, GATE_O]

    with ExitStack() as ctx:
        keep = ctx.enter_context(tc.tile_pool(name="keep", bufs=1))
        rows_pool = ctx.enter_context(tc.tile_pool(name="rows", bufs=2 * GATES))
        turned_pool = ctx.enter_context(tc.tile_pool(name="turned", bufs=2))
        stage = ctx.enter_context(tc.tile_pool(name="stage", bufs=4))
        hidden_pool = ctx.enter_context(tc.tile_pool(name="hidden", bufs=2))
        gates_pool = ctx.enter_context(tc.tile_pool(name="gates", bufs=4))
        kept_pool = ctx.enter_context(tc.tile_pool(name="kept", bufs=1))
        banks = ctx.enter_context(tc.psum_pool(name="banks", bufs=6))
        hidden_banks = ctx.enter_context(tc.psum_pool(name="hidden_banks", bufs=1))
        ctx.enter_context(tc.manual_schedule())

        ident = keep.tile([P, P], F32, name="ident")
        make_identity(nc, ident[:])
        ident_bf = keep.tile([P, P], BF16, name="ident_bf")
        make_identity(nc, ident_bf[:])
        planes_flat = keep.tile([P, PLANES_AT + GATES * PASSES * HIDDEN], U8, name="planes", align_bytes=256)
        planes = planes_flat[:, PLANES_AT:].rearrange("p (q g n) -> p q g n", q=GATES, g=PASSES)

        def zero_planes(q):
            at = PLANES_AT + q * PASSES * HIDDEN
            nc.vector.memset(planes_flat[:, at : at + PASSES * HIDDEN].bitcast(I32), 0)

        ones = keep.tile([P, P], BF16, name="ones")
        nc.vector.memset(ones[:], 1.0)
        zeros = keep.tile([P, BANK], BF16, name="zeros")
        nc.vector.memset(zeros[:], 0.0)
        bias_rows = keep.tile([P, GATES, HIDDEN], BF16, name="bias_rows")
        nc.vector.memset(bias_rows[:].rearrange("p q n -> p (q n)").bitcast(I32), 0)
        for q in gate_order:
            zero_planes(q)

        for q in gate_order[:2]:
            for quad in range(4):
                nc.gpsimd.dma_start(
                    out=planes[32 * quad : 32 * quad + 4, q, :, :].bitcast(F32),
                    in_=scales_in[q][:, 4 * quad : 4 * quad + 4, :].rearrange("g r n -> r g n").bitcast(F32),
                )

        def load_plane(n):
            q = gate_order[2 + n // 4]
            quad = n % 4
            nc.sync.dma_start(
                out=planes[32 * quad : 32 * quad + 4, q, :, :].bitcast(I32),
                in_=scales_in[q][:, 4 * quad : 4 * quad + 4, :].rearrange("g r n -> r g n").bitcast(I32),
            )

        h0_sb = keep.tile([P, HIDDEN], BF16, name="h0_sb")
        nc.sync.dma_start(out=h0_sb[:], in_=h0[0])

        hidden_rows = {}

        def load_gate_rows(c, q, first=0, last=HIDDEN):
            if first == 0:
                hidden_rows[(c, q)] = rows_pool.tile([P, ROW_TILES, HIDDEN], BF16, name="rows", tag="rows")
            nc.sync.dma_start(
                out=hidden_rows[(c, q)][:, :, first:last],
                in_=hidden_in[q][c * CHUNK : (c + 1) * CHUNK, first:last].rearrange("(a p) k -> p a k", p=P),
            )

        def load_hidden_rows(c):
            for q in range(GATES):
                load_gate_rows(c, q)

        w_codes = {}

        def load_gate_codes(c, q):
            codes = keep.tile([P, PASSES, CHUNK], U32, name="w_codes_%d_%d" % (c, q), align_bytes=256)
            packed = words_in[q].rearrange("g p n t -> p g (n t)")
            nc.sync.dma_start(
                out=codes[:].bitcast(I32),
                in_=packed[:, :, 4 * c * CHUNK : 4 * (c + 1) * CHUNK].bitcast(I32),
            )
            w_codes[(c, q)] = codes

        last_codes = {}

        def load_last_codes(a):
            first = LAST * CHUNK + a * HALF_UNITS
            for pair in range(2):
                last_codes[(a, pair)] = keep.tile([P, PASSES, CHUNK], U32, name="last_codes_%d_%d" % (a, pair), align_bytes=256)
                for r in range(2):
                    packed = words_in[2 * pair + r].rearrange("g p n t -> p g (n t)")
                    nc.sync.dma_start(
                        out=last_codes[(a, pair)][:, :, r * HALF_UNITS : (r + 1) * HALF_UNITS].bitcast(I32),
                        in_=packed[:, :, 4 * first : 4 * (first + HALF_UNITS)].bitcast(I32),
                    )

        def load_codes(c):
            for q in gate_order:
                load_gate_codes(c, q)

        def load_bias(b):
            q, r = divmod(b, 2)
            nc.sync.dma_start(out=bias_rows[r : r + 1, q, :], in_=bias_in[q][r].rearrange("n o -> o n"))

        x_duos = {}

        def load_inputs(d):
            x_duos[d] = keep.tile([P, DUO, FEATURES], BF16, name="x_duo_%d" % d)
            nc.sync.dma_start(out=x_duos[d][:], in_=inputs[:, DUO * d : DUO * (d + 1), :])

        load_gate_rows(0, 0)
        load_gate_rows(0, 1)
        for b in range(0, 5):
            load_bias(b)
        load_gate_rows(0, 2)
        load_gate_rows(0, 3)
        load_inputs(0)
        for b in range(5, 8):
            load_bias(b)
        load_plane(0)
        load_plane(1)
        for d in range(1, DUOS):
            load_inputs(d)
        for n in range(2, 7):
            load_plane(n)
        for q in range(GATES):
            load_gate_rows(1, q, 0, HIDDEN // 2)
        load_plane(7)
        load_codes(0)
        for q in range(GATES):
            load_gate_rows(1, q, HIDDEN // 2, HIDDEN)
        c0_sb = keep.tile([P, HIDDEN], BF16, name="c0_sb")
        nc.sync.dma_start(out=c0_sb[:], in_=c0[0])
        load_codes(1)
        load_hidden_rows(2)
        load_codes(2)
        load_hidden_rows(LAST)
        for a in range(HALVES):
            load_last_codes(a)

        def warm_up():
            bank = hidden_banks.tile([P, BANK], F32, name="warm_bank", tag="hidden_sum_1")
            nc.tensor.matmul(out=bank[:], lhsT=ones[:], rhs=zeros[:], start=True, stop=True)

        def turn_h0():
            bank = banks.tile([P, HIDDEN], BF16, name="h0_bank", tag="bank")
            for k in range(K_SLICES):
                nc.tensor.transpose(bank[:, k * P : (k + 1) * P], h0_sb[:, k * P : (k + 1) * P], ident_bf[:])
            h0_t = keep.tile([P, HIDDEN], BF16, name="h0_t")
            nc.vector.tensor_copy(out=h0_t[:], in_=bank[:])
            return h0_t

        turned = {}

        def new_turned(c):
            turned[c] = turned_pool.tile([P, K_SLICES, GATES * CHUNK], BF16, name="turned", tag="turned")

        def turn_block(c, k, q, a, bank, col):
            nc.tensor.transpose(bank[:, col : col + P], hidden_rows[(c, q)][:, a, k * P : (k + 1) * P], ident_bf[:])

        slice_banks = {}

        def turn_slice(c, k, blocks):
            for n in blocks:
                if n == 0:
                    slice_banks[k] = banks.tile([P, GATES * CHUNK], BF16, name="rows_bank", tag="bank")
                turn_block(c, k, n // ROW_TILES, n % ROW_TILES, slice_banks[k], n * P)
                if n == GATES * ROW_TILES - 1:
                    nc.scalar.copy(out=turned[c][:, k, :], in_=slice_banks[k][:])

        last_banks = {}

        def turn_last(n):
            a, rest = divmod(n, K_SLICES * GATES)
            k, q = divmod(rest, GATES)
            m = n % (2 * GATES)
            if m == 0:
                last_banks[0] = banks.tile([P, GATES * CHUNK], BF16, name="rows_bank", tag="bank")
            rows = hidden_rows[(LAST, q)]
            nc.tensor.transpose(last_banks[0][:, m * P : (m + 1) * P], rows[:, a, k * P : (k + 1) * P], ident_bf[:])
            if m == 2 * GATES - 1:
                at = (a * K_SLICES + k - 1) * BANK
                nc.scalar.copy(
                    out=turned[LAST][:].rearrange("p k n -> p (k n)")[:, at : at + 2 * BANK], in_=last_banks[0][:]
                )

        def add_last_piece(n, r):
            a, k = divmod(n, K_SLICES)
            if k == 0 and r == 0:
                hidden_sum[(LAST, a)] = hidden_banks.tile([P, BANK], F32, name="hidden_sum_%d" % a)
            at = (a * K_SLICES + k) * BANK + r * CHUNK
            nc.tensor.matmul(
                out=hidden_sum[(LAST, a)][:, r * CHUNK : (r + 1) * CHUNK],
                lhsT=h0_t[:, k * P : (k + 1) * P],
                rhs=turned[LAST][:].rearrange("p k n -> p (k n)")[:, at : at + CHUNK],
                start=(k == 0 and r == 0),
                stop=False,
            )
            if k == K_SLICES - 1 and r == 1:
                first = LAST * CHUNK + a * HALF_UNITS
                nc.tensor.matmul(
                    out=hidden_sum[(LAST, a)][:],
                    lhsT=ones[:],
                    rhs=bias_rows[:, :, first : first + HALF_UNITS],
                    start=False,
                    stop=True,
                )

        hidden_sum = {}

        def close_hidden_sum(c, half):
            nc.tensor.matmul(
                out=hidden_sum[(c, half)][:],
                lhsT=ones[:],
                rhs=bias_rows[:, 2 * half : 2 * half + 2, c * CHUNK : (c + 1) * CHUNK],
                start=False,
                stop=True,
            )

        def add_hidden_slice(c, k, half):
            if k == 0:
                hidden_sum[(c, half)] = hidden_banks.tile([P, BANK], F32, name="hidden_sum_%d" % half)
            nc.tensor.matmul(
                out=hidden_sum[(c, half)][:],
                lhsT=h0_t[:, k * P : (k + 1) * P],
                rhs=turned[c][:, k, half * BANK : (half + 1) * BANK],
                start=(k == 0),
                stop=False,
            )

        def hidden_sum_out(c):
            hidden_sb = hidden_pool.tile([P, GATES * CHUNK], F32, name="hidden_sb", tag="hidden_sb")
            for half in range(HALVES):
                nc.vector.tensor_copy(out=hidden_sb[:, half * BANK : (half + 1) * BANK], in_=hidden_sum[(c, half)][:])
            return hidden_sb

        sorted_duos = {}

        def sort_inputs(d):
            sorted_duos[d] = keep.tile([P, DUO * FEATURES // 2], F32, name="sorted_%d" % d)
            nc.vector.tensor_copy(
                out=sorted_duos[d][:].rearrange("p (a u b) -> p a u b", u=2, b=P),
                in_=x_duos[d][:].rearrange("p s k -> p (s k)").bitcast(F32).rearrange("p (a b u) -> p a u b", u=2, b=P),
            )

        def turn_inputs(t, g, bank):
            for u in range(2):
                col = (2 * g + u) * P
                at = ((t % DUO) * PASSES * 2 + 2 * g + u) * P
                nc.tensor.transpose(bank[:, col : col + P], sorted_duos[t // DUO][:, at : at + P], ident[:])

        def group_inputs(bank):
            grouped = stage.tile([P, FEATURES], BF16, name="grouped", align_bytes=64)
            nc.scalar.copy(
                out=grouped[:].bitcast(F32).rearrange("p (g b u) -> p g b u", g=PASSES, u=2),
                in_=bank[:].rearrange("p (g u b) -> p g b u", g=PASSES, u=2),
            )
            return grouped

        x_codes = {}
        x_scales = {}

        def quantise_inputs(t, grouped):
            codes = keep.tile([P, X_CODES_AT + PASSES * P], U32, name="x_codes_%d" % t, align_bytes=256)
            scales = keep.tile([P, X_SCALES_AT + PASSES * P], U8, name="x_scales_%d" % t, align_bytes=256)
            x_codes[t] = codes[:, X_CODES_AT:]
            x_scales[t] = scales[:, X_SCALES_AT:]
            nc.vector.quantize_mx(out=x_codes[t].bitcast(FP8X4), scales=x_scales[t], in_=grouped[:])

        def gate_sums(r, q, hidden_sb, z_sb):
            first, width, t0, steps = r
            c, at = divmod(first, CHUNK)
            bank = banks.tile([P, BANK], F32, name="z_bank", tag="bank")
            for s in range(steps):
                for g in range(PASSES):
                    nc.tensor.matmul_mx(
                        out=bank[:, s * width : (s + 1) * width],
                        lhsT=x_codes[t0 + s][:, g * P : (g + 1) * P].bitcast(FP8X4),
                        lhsT_scale=x_scales[t0 + s][:, g * P : (g + 1) * P],
                        rhs=w_codes[(c, q)][:, g, at : at + width].bitcast(FP8X4),
                        rhs_scale=planes[:, q, g, first : first + width],
                        start=(g == 0),
                        stop=(g == PASSES - 1),
                    )
            nc.vector.tensor_tensor(
                out=z_sb[:, q, :, :],
                in0=bank[:].rearrange("p (s n) -> p s n", s=steps),
                in1=hidden_sb[:, q * width : (q + 1) * width].unsqueeze(1).to_broadcast([P, steps, width]),
                op=ALU.add,
            )

        last_planes = {}

        def place_last_planes(a):
            first = LAST * CHUNK + a * HALF_UNITS
            for pair in range(2):
                flat = keep.tile([P, PLANES_AT + PASSES * CHUNK], U8, name="last_planes_%d_%d" % (a, pair), align_bytes=256)
                last_planes[(a, pair)] = flat[:, PLANES_AT:].rearrange("p (g n) -> p g n", g=PASSES)
                for r in range(2):
                    nc.vector.tensor_copy(
                        out=last_planes[(a, pair)][:, :, r * HALF_UNITS : (r + 1) * HALF_UNITS].bitcast(I32),
                        in_=planes[:, 2 * pair + r, :, first : first + HALF_UNITS].bitcast(I32),
                    )

        def pair_sums(a, t0, pair, hidden_sb, z_out):
            bank = banks.tile([P, BANK], F32, name="z_bank", tag="bank")
            for s in range(DUO):
                for g in range(PASSES):
                    nc.tensor.matmul_mx(
                        out=bank[:, s * CHUNK : (s + 1) * CHUNK],
                        lhsT=x_codes[t0 + s][:, g * P : (g + 1) * P].bitcast(FP8X4),
                        lhsT_scale=x_scales[t0 + s][:, g * P : (g + 1) * P],
                        rhs=last_codes[(a, pair)][:, g, :].bitcast(FP8X4),
                        rhs_scale=last_planes[(a, pair)][:, g, :],
                        start=(g == 0),
                        stop=(g == PASSES - 1),
                    )
            nc.vector.tensor_tensor(
                out=z_out,
                in0=bank[:].rearrange("p (s n) -> p s n", s=DUO),
                in1=hidden_sb[:, pair * CHUNK : (pair + 1) * CHUNK].unsqueeze(1).to_broadcast([P, DUO, CHUNK]),
                op=ALU.add,
            )

        def gate_of(z_sb, q, width):
            if width == CHUNK:
                return z_sb[:, q, :, :]
            pair, r = divmod(q, 2)
            return z_sb[:, pair, :, r * HALF_UNITS : (r + 1) * HALF_UNITS]

        def activate(z_sb, q):
            nc.scalar.activation(out=z_sb[:, q, :, :], in_=z_sb[:, q, :, :], func=(ACT.Tanh if q == GATE_G else ACT.Sigmoid))

        def cell_products(r, z_sb, engine):
            first, width, t0, steps = r
            c0_chunk = c0_sb[:, first : first + width].unsqueeze(1).to_broadcast([P, steps, width])
            kept = kept_pool.tile([P, steps, width], F32, name="kept")
            i_gate = gate_of(z_sb, GATE_I, width)
            engine.tensor_tensor(out=kept[:], in0=gate_of(z_sb, GATE_F, width), in1=c0_chunk, op=ALU.mult)
            engine.tensor_tensor(out=i_gate, in0=i_gate, in1=gate_of(z_sb, GATE_G, width), op=ALU.mult)
            return kept

        def cell_state(r, z_sb, kept):
            first, width, t0, steps = r
            cell = stage.tile([P, steps, width], F32, name="cell", bufs=2)
            nc.vector.tensor_tensor(out=cell[:], in0=kept, in1=gate_of(z_sb, GATE_I, width), op=ALU.add)
            if t0 + steps == STEPS:
                nc.sync.dma_start(out=out_2[0, :, first : first + width], in_=cell[:, steps - 1, :])
            return cell

        def cell_tanh(r, z_sb, cell):
            nc.scalar.activation(out=gate_of(z_sb, GATE_G, r[1]), in_=cell[:], func=ACT.Tanh)

        def hidden_state(r, z_sb):
            first, width, t0, steps = r
            cols = slice(first, first + width)
            h_sb = stage.tile([P, steps, width], F32, name="h_sb")
            nc.vector.tensor_tensor(out=h_sb[:], in0=gate_of(z_sb, GATE_O, width), in1=gate_of(z_sb, GATE_G, width), op=ALU.mult)
            nc.sync.dma_start(out=out_0[t0 : t0 + steps, :, cols].rearrange("t b n -> b t n"), in_=h_sb[:])
            if t0 + steps == STEPS:
                nc.sync.dma_start(out=out_1[0, :, cols], in_=h_sb[:, steps - 1, :])

        for n in range(WARM_FIRST):
            warm_up()
        h0_t = turn_h0()
        for d in range(DUOS):
            sort_inputs(d)

        new_turned(0)
        first_banks = {}
        FOUR = K_SLICES // 2

        def turn_first(q, k):
            if k % FOUR == 0:
                first_banks[q] = banks.tile([P, FOUR, CHUNK], BF16, name="rows_bank", tag="bank")
            for a in range(ROW_TILES):
                nc.tensor.transpose(
                    first_banks[q][:, k % FOUR, a * P : (a + 1) * P],
                    hidden_rows[(0, q)][:, a, k * P : (k + 1) * P],
                    ident_bf[:],
                )
            if k % FOUR == FOUR - 1:
                nc.scalar.copy(out=turned[0][:, k - FOUR + 1 : k + 1, q * CHUNK : (q + 1) * CHUNK], in_=first_banks[q][:])

        for q in range(2):
            for k in range(K_SLICES):
                turn_first(q, k)
                if k % FOUR == FOUR - 1:
                    warm_up()
        grouped_of = {}
        x_banks = {}

        def turn_next_inputs(job):
            t, g = divmod(job, PASSES)
            if g == 0:
                x_banks[t] = banks.tile([P, BANK], F32, name="x_bank", tag="bank")
            turn_inputs(t, g, x_banks[t])
            if g == PASSES - 1:
                grouped_of[t] = group_inputs(x_banks[t])
                if t > 0:
                    quantise_inputs(t - 1, grouped_of[t - 1])

        for k in range(K_SLICES):
            add_hidden_slice(0, k, 0)
            turn_first(2 + k // FOUR, 2 * (k % FOUR))
            turn_first(2 + k // FOUR, 2 * (k % FOUR) + 1)
        for k in range(K_SLICES):
            add_hidden_slice(0, k, 1)
            turn_next_inputs(2 * k)
            turn_next_inputs(2 * k + 1)
        close_hidden_sum(0, 0)
        close_hidden_sum(0, 1)
        quantise_inputs(STEPS - 1, grouped_of[STEPS - 1])
        new_turned(1)
        for k in range(2):
            turn_slice(1, k, range(GATES * ROW_TILES))

        rounds = [(c * CHUNK, CHUNK, DUO * d, DUO) for c in range(LAST) for d in range(DUOS)]
        rounds += [
            (LAST * CHUNK + a * HALF_UNITS, HALF_UNITS, QUAD * d, QUAD) for a in range(HALVES) for d in range(QUADS)
        ]
        count = len(rounds)
        z_of = {}
        kept_of = {}
        cell_of = {}
        hidden_sb = None
        blocks = GATES * ROW_TILES
        last_jobs = {
            7: ([], range(0, 8)),
            8: (range(0, 2), range(8, 16)),
            9: (range(2, 4), range(16, 32)),
            10: (range(4, 8), range(32, 40)),
            11: (range(8, 10), range(40, 56)),
            12: (range(10, 12), range(56, 64)),
            13: (range(12, 16), range(0)),
        }

        def prepare(j):
            c, d = divmod(j, DUOS)
            adds = []
            turns = []
            if c + 1 < LAST:
                adds = [lambda k=2 * d + m % 2, half=m // 2: add_hidden_slice(c + 1, k, half) for m in range(4)]
            next_c, next_d = divmod(j + DUOS + 1, DUOS)
            if next_c < LAST:
                if next_d == 0:
                    new_turned(next_c)
                turns = [lambda n=n: turn_slice(next_c, 2 * next_d + n // blocks, [n % blocks]) for n in range(2 * blocks)]
            if j in last_jobs:
                if j == 7:
                    new_turned(LAST)
                adds += [lambda n=n, r=r: add_last_piece(n, r) for n in last_jobs[j][0] for r in range(2)]
                turns += [lambda n=n: turn_last(n) for n in last_jobs[j][1]]
            gaps = len(adds) - 1
            for m in range(len(adds)):
                adds[m]()
                if m < gaps:
                    for turn in turns[len(turns) * m // gaps : len(turns) * (m + 1) // gaps]:
                        turn()
            if c + 1 < LAST and d == DUOS - 1:
                close_hidden_sum(c + 1, 0)
                close_hidden_sum(c + 1, 1)

        half_sums = {}

        def half_sum_out(a, copy):
            half_sums[a] = hidden_pool.tile([P, GATES * CHUNK], F32, name="hidden_sb", tag="hidden_sb")
            copy(out=half_sums[a][:, 0:BANK], in_=hidden_sum[(LAST, a)][:])

        for a in range(HALVES):
            place_last_planes(a)
        for j in range(count):
            c = rounds[j][0] // CHUNK
            if j >= 1:
                kept_of[j - 1] = cell_products(rounds[j - 1], z_of[j - 1], nc.gpsimd)
            if rounds[j][2] == 0:
                if c < LAST:
                    hidden_sb = hidden_sum_out(c)
                else:
                    if j == count - QUADS:
                        half_sum_out(1, nc.vector.tensor_copy)
                    hidden_sb = half_sums[rounds[j][0] % CHUNK // HALF_UNITS]
            if c < LAST:
                z_of[j] = gates_pool.tile([P, GATES, DUO, CHUNK], F32, name="z_sb", tag="z_sb")
                for q in gate_order:
                    gate_sums(rounds[j], q, hidden_sb, z_of[j])
                    activate(z_of[j], q)
            else:
                z_of[j] = gates_pool.tile([P, 2, QUAD, CHUNK], F32, name="z_sb", tag="z_sb")
                a = rounds[j][0] % CHUNK // HALF_UNITS
                for s in range(0, QUAD, DUO):
                    pair_sums(a, rounds[j][2] + s, 0, hidden_sb, z_of[j][:, 0, s : s + DUO, :])
                    pair = z_of[j][:, 0, s : s + DUO, :]
                    nc.scalar.activation(out=pair, in_=pair, func=ACT.Sigmoid)
                for s in range(0, QUAD, DUO):
                    pair_sums(a, rounds[j][2] + s, 1, hidden_sb, z_of[j][:, 1, s : s + DUO, :])
                for q in (GATE_G, GATE_O):
                    gate = gate_of(z_of[j], q, HALF_UNITS)
                    nc.scalar.activation(out=gate, in_=gate, func=(ACT.Tanh if q == GATE_G else ACT.Sigmoid))
            if j == LAST * DUOS - 1:
                half_sum_out(0, nc.scalar.copy)
            prepare(j)
            if j >= 1:
                cell_of[j - 1] = cell_state(rounds[j - 1], z_of[j - 1], kept_of[j - 1][:])
                cell_tanh(rounds[j - 1], z_of[j - 1], cell_of[j - 1])
            if j >= 2:
                hidden_state(rounds[j - 2], z_of[j - 2])

        last = count - 1
        kept_of[last] = cell_products(rounds[last], z_of[last], nc.vector)
        first, width, t0, steps = rounds[last]
        parts = []
        for s in range(0, QUAD, DUO):
            part = (first, width, t0 + s, DUO)
            z_part = z_of[last][:, :, s : s + DUO, :]
            cell = cell_state(part, z_part, kept_of[last][:, s : s + DUO, :])
            cell_tanh(part, z_part, cell)
            parts.append((part, z_part))
        hidden_state(rounds[last - 1], z_of[last - 1])
        for part, z_part in parts:
            hidden_state(part, z_part)
